import numpy as np
import ml_dtypes


def mxq(x, axis, fmt="e4m3"):
    dtype, down = {"e4m3": (ml_dtypes.float8_e4m3fn, 7), "e5m2": (ml_dtypes.float8_e5m2, 14)}[fmt]
    v = np.moveaxis(np.asarray(x, np.float32).astype(ml_dtypes.bfloat16).astype(np.float64), axis, -1)
    blocks = v.reshape(v.shape[:-1] + (-1, 32))
    amax = np.abs(blocks).max(-1, keepdims=True)
    byte = np.maximum(np.where(amax > 0, np.frexp(amax)[1] - 1 + 127, 0) - down, 1)
    scale = np.exp2(byte - 127.0)
    codes = (blocks / scale).astype(np.float32).astype(dtype).astype(np.float64)
    return np.moveaxis((codes * scale).reshape(v.shape), -1, axis)


WIDE = False


def mx_kscale(k):
    if not WIDE:
        return np.ones(k)
    levels = np.array([10, -10, 5, -5, 0])
    a = np.random.permutation(np.resize(levels, k // 512 * 4)).reshape(k // 512, 4)
    idx = np.arange(k)
    return np.exp2(a[idx // 512, idx % 128 // 32])


BF16 = ml_dtypes.bfloat16


def bf(x):
    return np.asarray(x, np.float32).astype(BF16)


def f64(x):
    return np.asarray(x).astype(np.float64)


E, T, H, D, R = 4, 256, 1024, 1024, 128
SCALE = 2.0


def silu(v):
    return v / (1.0 + np.exp(-v))


def setup_inputs():
    s = mx_kscale(H)
    return {"x": bf(np.random.standard_normal((E, T, H)) * s),
            "low_gu": bf(np.random.standard_normal((E, T, R))),
            "W_gu": bf(np.random.standard_normal((E, 2 * D, H)) / np.sqrt(H) / s),
            "B_gu": bf(np.random.standard_normal((E, 2 * D, R)) * 0.3 / np.sqrt(R)),
            "A_d": bf(np.random.standard_normal((E, R, D)) * 1.5 / np.sqrt(D))}


def reference(x, low_gu, W_gu, B_gu, A_d):
    base = mxq(f64(x), 2, "e4m3") @ mxq(f64(W_gu), 2, "e4m3").transpose(0, 2, 1)
    delta = f64(low_gu) @ f64(B_gu).transpose(0, 2, 1)
    gate_up = base + SCALE * delta
    gate, up = gate_up[..., :D], gate_up[..., D:]
    h = up * silu(gate)
    low_d = mxq(h, 2, "e4m3") @ mxq(f64(A_d), 2, "e4m3").transpose(0, 2, 1)
    return h, low_d

@@ -1,0 +1,283 @@
+from contextlib import ExitStack
+
+import concourse.mybir as mybir
+from concourse.masks import make_identity
+
+F32 = mybir.dt.float32
+BF16 = mybir.dt.bfloat16
+U32 = mybir.dt.uint32
+U8 = mybir.dt.uint8
+FP8X4 = mybir.dt.float8_e4m3fn_x4
+ACT = mybir.ActivationFunctionType
+ALU = mybir.AluOpType
+
+E, T, H, D, R = 4, 256, 1024, 1024, 128
+P = 128
+FLOPS = 2 * E * T * (2 * D * H + 2 * D * R + D * R)
+
+W_BUFS = 6
+UNITS = 2 * E
+
+
+def tile_loralinearexpertswrapper_pa_kernel(tc, x, low_gu, W_gu, B_gu, A_d, out_0, out_1):
+    nc = tc.nc
+    with ExitStack() as ctx:
+        const = ctx.enter_context(tc.tile_pool(name="const", bufs=1))
+        sb = ctx.enter_context(tc.tile_pool(name="sb", bufs=2))
+        ps = ctx.enter_context(tc.psum_pool(name="ps", bufs=2))
+
+        ident32 = const.tile([P, P], F32, name="ident32")
+        make_identity(nc, ident32[:])
+        identb = const.tile([P, P], BF16, name="identb")
+        make_identity(nc, identb[:])
+
+        state = {"evac": 0}
+
+        def evac(out, in_, who=None):
+            if who is None:
+                who = "v" if state["evac"] % 2 == 0 else "s"
+                state["evac"] += 1
+            if who == "v":
+                nc.vector.tensor_copy(out=out, in_=in_)
+            else:
+                nc.scalar.copy(out=out, in_=in_)
+
+        w_raw = {}
+        x_raw = {}
+        b_raw = {}
+
+        def load_w(n, s):
+            if n >= UNITS:
+                return
+            e, j = divmod(n, 2)
+            t = sb.tile([P, 4, H], BF16, name="w_raw", tag="w_raw", bufs=W_BUFS)
+            r0 = D * s + 512 * j
+            nc.sync.dma_start(out=t[:], in_=W_gu[e, r0:r0 + 512, :].rearrange("(p c) k -> p c k", c=4))
+            w_raw[(n, s)] = t
+
+        def load_x(e):
+            t = sb.tile([P, 2, H], BF16, name="x_raw", tag="x_raw", bufs=2)
+            nc.sync.dma_start(out=t[:], in_=x[e].rearrange("(p m) k -> p m k", m=2))
+            x_raw[e] = t
+
+        def load_b(e):
+            t = sb.tile([P, 4, 4, R], BF16, name="b_raw", tag="b_raw", bufs=2)
+            nc.sync.dma_start(out=t[:], in_=B_gu[e].rearrange("(q p c) r -> p q c r", p=P, c=4))
+            b_raw[e] = t
+
+        x_q = {}
+        w_q = {}
+        b_t = {}
+        a_q = {}
+
+        def prep_x(e):
+            x32 = x_raw[e][:].bitcast(F32)
+            xg = sb.tile([P, 2, T, 4], BF16, name="xg", tag="xg", bufs=2, align_bytes=64)
+            xg32 = xg[:].bitcast(F32)
+            for g in range(2):
+                xt = ps.tile([P, 2, T], F32, name="xt", tag="tw", bufs=4)
+                for u in range(2):
+                    for m in range(2):
+                        k0 = 256 * g + 128 * u
+                        nc.tensor.transpose(xt[:, u, m * P:(m + 1) * P], x32[:, m, k0:k0 + P], ident32[:])
+                evac(xg32[:, g, :, :], xt[:].rearrange("q u r -> q r u"))
+            xc = sb.tile([P, 2, T], U32, name="xc", tag="xc", bufs=2, align_bytes=64)
+            xs = sb.tile([P, 2, T], U8, name="xs", tag="xs", bufs=2, align_bytes=64)
+            nc.vector.quantize_mx(
+                out=xc[:].rearrange("q g r -> q (g r)").bitcast(FP8X4),
+                scales=xs[:].rearrange("q g r -> q (g r)"),
+                in_=xg[:].rearrange("q g r t -> q (g r t)"),
+            )
+            x_q[e] = (xc, xs)
+
+        def prep_w(n, s):
+            if n >= UNITS:
+                return
+            w32 = w_raw[(n, s)][:].bitcast(F32)
+            wg = sb.tile([P, 2, 512, 4], BF16, name="wg", tag="wg", bufs=3, align_bytes=64)
+            wg32 = wg[:].bitcast(F32)
+            for g in range(2):
+                for cp in range(2):
+                    wt = ps.tile([P, 2, 256], F32, name="wt", tag="tw", bufs=4)
+                    for u in range(2):
+                        for c2 in range(2):
+                            k0 = 256 * g + 128 * u
+                            nc.tensor.transpose(
+                                wt[:, u, c2 * P:(c2 + 1) * P], w32[:, 2 * cp + c2, k0:k0 + P], ident32[:]
+                            )
+                    evac(wg32[:, g, cp * 256:(cp + 1) * 256, :], wt[:].rearrange("q u r -> q r u"))
+            wc = sb.tile([P, 2, 512], U32, name="wc", tag="wc", bufs=4, align_bytes=64)
+            ws = sb.tile([P, 2, 512], U8, name="ws", tag="ws", bufs=4, align_bytes=64)
+            nc.vector.quantize_mx(
+                out=wc[:].rearrange("q g r -> q (g r)").bitcast(FP8X4),
+                scales=ws[:].rearrange("q g r -> q (g r)"),
+                in_=wg[:].rearrange("q g r t -> q (g r t)"),
+            )
+            w_q[(n, s)] = (wc, ws)
+
+        def prep_b(e):
+            bt = sb.tile([P, 4, 512], BF16, name="bt", tag="bt", bufs=2)
+            for half in range(2):
+                bp = ps.tile([P, 2, 512], BF16, name="bp", tag="tw", bufs=4)
+                for q2 in range(2):
+                    for c in range(4):
+                        nc.tensor.transpose(
+                            bp[:, q2, c * P:(c + 1) * P], b_raw[e][:, 2 * half + q2, c, :], identb[:]
+                        )
+                evac(bt[:, 2 * half:2 * half + 2, :], bp[:], "s")
+            b_t[e] = bt
+
+        def prep_a(e):
+            ap_ = ps.tile([P, 2, 4, R], BF16, name="ap_", tag="tw", bufs=4)
+            for g in range(2):
+                for t4 in range(4):
+                    k0 = 512 * g + 128 * t4
+                    nc.tensor.transpose(ap_[:, g, t4, :], a_raw[:, e, k0:k0 + P], identb[:])
+            ag = sb.tile([P, 2, R, 4], BF16, name="ag", tag="ag", bufs=2, align_bytes=64)
+            evac(ag[:], ap_[:].rearrange("p g t r -> p g r t"), "s")
+            ac = sb.tile([P, 2, R], U32, name="ac", tag="ac", bufs=2, align_bytes=64)
+            asc = sb.tile([P, 2, R], U8, name="asc", tag="asc", bufs=2, align_bytes=64)
+            nc.vector.quantize_mx(
+                out=ac[:].rearrange("q g r -> q (g r)").bitcast(FP8X4),
+                scales=asc[:].rearrange("q g r -> q (g r)"),
+                in_=ag[:].rearrange("q g r t -> q (g r t)"),
+            )
+            a_q[e] = (ac, asc)
+
+        d_sb = {}
+        h_sb = {}
+        h_q = {}
+
+        def delta(n, m):
+            e, j = divmod(n, 2)
+            for s in range(2):
+                pd = ps.tile([P, 512], F32, name="pd", tag="pd", bufs=2)
+                nc.tensor.matmul(pd[:], lhsT=low_t[:, e, m, :], rhs=b_t[e][:, 2 * s + j, :], start=True, stop=True)
+                dt_ = sb.tile([P, 512], F32, name="dt_", tag="dt_", bufs=6)
+                evac(
+                    dt_[:].rearrange("t (p c) -> t p c", c=4),
+                    pd[:].rearrange("t (c p) -> t p c", c=4),
+                    "s",
+                )
+                d_sb[(n, m, s)] = dt_
+
+        def base(n, m):
+            e, j = divmod(n, 2)
+            xc, xs = x_q[e]
+            sums = []
+            for s in range(2):
+                wc, ws = w_q[(n, s)]
+                pb = ps.tile([P, 512], F32, name="pb", tag="pb", bufs=2)
+                for g in range(2):
+                    nc.tensor.matmul_mx(
+                        out=pb[:],
+                        lhsT=xc[:, g, m * P:(m + 1) * P].bitcast(FP8X4),
+                        lhsT_scale=xs[:, g, m * P:(m + 1) * P],
+                        rhs=wc[:, g, :].bitcast(FP8X4),
+                        rhs_scale=ws[:, g, :],
+                        start=(g == 0),
+                        stop=(g == 1),
+                    )
+                gu = sb.tile([P, 512], F32, name="gu", tag="gu%d" % s, bufs=2)
+                nc.vector.tensor_tensor(
+                    out=gu[:].rearrange("t (p c) -> t p c", c=4),
+                    in0=pb[:].rearrange("t (c p) -> t p c", c=4),
+                    in1=d_sb[(n, m, s)][:].rearrange("t (p c) -> t p c", c=4),
+                    op=ALU.add,
+                )
+                sums.append(gu)
+            sl = sb.tile([P, 512], F32, name="sl", tag="sl", bufs=2)
+            nc.scalar.activation(out=sl[:], in_=sums[0][:], func=ACT.Silu)
+            if m == 0:
+                h_new = sb.tile([P, 2, 512], F32, name="h_new", tag="h", bufs=3)
+                h_sb[n] = h_new
+            nc.vector.tensor_tensor(out=h_sb[n][:, m, :], in0=sums[1][:], in1=sl[:], op=ALU.mult)
+
+        def store_h(n):
+            e, j = divmod(n, 2)
+            nc.gpsimd.dma_start(
+                out=out_0[e, :, 512 * j:512 * (j + 1)].rearrange("(p m) d -> p m d", m=2), in_=h_sb[n][:]
+            )
+
+        def h_t(n):
+            e, j = divmod(n, 2)
+            hg = sb.tile([P, T, 4], BF16, name="hg", tag="hg", bufs=2, align_bytes=64)
+            for m in range(2):
+                hp = ps.tile([P, 4, P], F32, name="hp", tag="tw", bufs=4)
+                for t4 in range(4):
+                    nc.tensor.transpose(hp[:, t4, :], h_sb[n][:, m, t4 * P:(t4 + 1) * P], ident32[:])
+                evac(hg[:, m * P:(m + 1) * P, :], hp[:].rearrange("p t r -> p r t"), "s")
+            if j == 0:
+                hc_new = sb.tile([P, 2, T], U32, name="hc_new", tag="hc", bufs=2, align_bytes=64)
+                hs_new = sb.tile([P, 2, T], U8, name="hs_new", tag="hs", bufs=2, align_bytes=64)
+                h_q[e] = (hc_new, hs_new)
+            hc, hs = h_q[e]
+            nc.vector.quantize_mx(
+                out=hc[:, j, :].bitcast(FP8X4), scales=hs[:, j, :], in_=hg[:].rearrange("p r t -> p (r t)")
+            )
+
+        def low_d(e):
+            hc, hs = h_q[e]
+            ac, asc = a_q[e]
+            pl = ps.tile([P, 2, R], F32, name="pl", tag="pd", bufs=2)
+            for m in range(2):
+                for g in range(2):
+                    nc.tensor.matmul_mx(
+                        out=pl[:, m, :],
+                        lhsT=hc[:, g, m * P:(m + 1) * P].bitcast(FP8X4),
+                        lhsT_scale=hs[:, g, m * P:(m + 1) * P],
+                        rhs=ac[:, g, :].bitcast(FP8X4),
+                        rhs_scale=asc[:, g, :],
+                        start=(g == 0),
+                        stop=(g == 1),
+                    )
+            lo = sb.tile([P, 2, R], F32, name="lo", tag="lo", bufs=2)
+            evac(lo[:], pl[:], "s")
+            nc.gpsimd.dma_start(out=out_1[e].rearrange("(p m) r -> p m r", m=2), in_=lo[:])
+
+        load_x(0)
+        load_w(0, 0)
+        load_w(0, 1)
+        low_raw = const.tile([P, E, 2, R], BF16, name="low_raw")
+        nc.sync.dma_start(out=low_raw[:], in_=low_gu.rearrange("e (p m) r -> p e m r", m=2))
+        load_b(0)
+        load_w(1, 0)
+        load_w(1, 1)
+        a_raw = const.tile([P, E, D], BF16, name="a_raw")
+        nc.sync.dma_start(out=a_raw[:], in_=A_d.rearrange("e r d -> r e d"))
+        load_w(2, 0)
+        load_w(2, 1)
+
+        prep_x(0)
+        prep_w(0, 0)
+        prep_w(0, 1)
+        lp = ps.tile([P, E, 2, P], BF16, name="lp", tag="tw", bufs=4)
+        for e in range(E):
+            for m in range(2):
+                nc.tensor.transpose(lp[:, e, m, :], low_raw[:, e, m, :], identb[:])
+        low_t = const.tile([P, E, 2, P], BF16, name="low_t")
+        nc.scalar.mul(out=low_t[:], in_=lp[:], mul=2.0)
+        prep_b(0)
+
+        for n in range(UNITS):
+            e, j = divmod(n, 2)
+            if j == 0 and e + 1 < E:
+                load_x(e + 1)
+                load_b(e + 1)
+            load_w(n + 3, 0)
+            load_w(n + 3, 1)
+            delta(n, 0)
+            prep_w(n + 1, 0)
+            base(n, 0)
+            delta(n, 1)
+            prep_w(n + 1, 1)
+            base(n, 1)
+            store_h(n)
+            if j == 0:
+                prep_a(e)
+            if j == 0 and e + 1 < E:
+                prep_x(e + 1)
+                prep_b(e + 1)
+            h_t(n)
+            if j == 1:
+                low_d(e)

@@ -15,8 +15,10 @@ E, T, H, D, R = 4, 256, 1024, 1024, 128
 P = 128
 FLOPS = 2 * E * T * (2 * D * H + 2 * D * R + D * R)
 
+LW = 2
 W_BUFS = 6
-UNITS = 2 * E
+PHASES = 4 * E
+CHUNKS = 4 * E
 
 
 def tile_loralinearexpertswrapper_pa_kernel(tc, x, low_gu, W_gu, B_gu, A_d, out_0, out_1):
@@ -25,198 +27,276 @@ def tile_loralinearexpertswrapper_pa_kernel(tc, x, low_gu, W_gu, B_gu, A_d, out_
         const = ctx.enter_context(tc.tile_pool(name="const", bufs=1))
         sb = ctx.enter_context(tc.tile_pool(name="sb", bufs=2))
         ps = ctx.enter_context(tc.psum_pool(name="ps", bufs=2))
+        ctx.enter_context(tc.manual_schedule())
 
         ident32 = const.tile([P, P], F32, name="ident32")
         make_identity(nc, ident32[:])
         identb = const.tile([P, P], BF16, name="identb")
         make_identity(nc, identb[:])
+        low_raw = const.tile([P, E, 2, R], BF16, name="low_raw")
+        low_t = const.tile([P, E, 2, P], BF16, name="low_t")
+        a_raw = const.tile([P, E, D], BF16, name="a_raw")
 
-        state = {"evac": 0}
-
-        def evac(out, in_, who=None):
-            if who is None:
-                who = "v" if state["evac"] % 2 == 0 else "s"
-                state["evac"] += 1
+        def evac(who, out, in_):
             if who == "v":
                 nc.vector.tensor_copy(out=out, in_=in_)
             else:
                 nc.scalar.copy(out=out, in_=in_)
 
-        w_raw = {}
-        x_raw = {}
-        b_raw = {}
+        w_raw, x_raw, b_raw = {}, {}, {}
+        bank = {}
+        wg, xg, ag, hg = {}, {}, {}, {}
+        x_q, w_q, b_t, a_q, h_q = {}, {}, {}, {}, {}
+        d_sb, gu, sl, h_sb = {}, {}, {}, {}
 
-        def load_w(n, s):
-            if n >= UNITS:
+        def tw_bank(shape, dtype):
+            return ps.tile(shape, dtype, name="tw", tag="tw", bufs=4)
+
+        def load_w(c):
+            if c < 0 or c >= CHUNKS:
                 return
+            n, s = divmod(c, 2)
             e, j = divmod(n, 2)
             t = sb.tile([P, 4, H], BF16, name="w_raw", tag="w_raw", bufs=W_BUFS)
             r0 = D * s + 512 * j
             nc.sync.dma_start(out=t[:], in_=W_gu[e, r0:r0 + 512, :].rearrange("(p c) k -> p c k", c=4))
-            w_raw[(n, s)] = t
+            w_raw[c] = t
 
         def load_x(e):
+            if e >= E:
+                return
             t = sb.tile([P, 2, H], BF16, name="x_raw", tag="x_raw", bufs=2)
             nc.sync.dma_start(out=t[:], in_=x[e].rearrange("(p m) k -> p m k", m=2))
             x_raw[e] = t
 
         def load_b(e):
+            if e >= E:
+                return
             t = sb.tile([P, 4, 4, R], BF16, name="b_raw", tag="b_raw", bufs=2)
             nc.sync.dma_start(out=t[:], in_=B_gu[e].rearrange("(q p c) r -> p q c r", p=P, c=4))
             b_raw[e] = t
 
-        x_q = {}
-        w_q = {}
-        b_t = {}
-        a_q = {}
-
-        def prep_x(e):
+        def tx(e, g):
+            if e < 0 or e >= E:
+                return
             x32 = x_raw[e][:].bitcast(F32)
-            xg = sb.tile([P, 2, T, 4], BF16, name="xg", tag="xg", bufs=2, align_bytes=64)
-            xg32 = xg[:].bitcast(F32)
-            for g in range(2):
-                xt = ps.tile([P, 2, T], F32, name="xt", tag="tw", bufs=4)
-                for u in range(2):
-                    for m in range(2):
-                        k0 = 256 * g + 128 * u
-                        nc.tensor.transpose(xt[:, u, m * P:(m + 1) * P], x32[:, m, k0:k0 + P], ident32[:])
-                evac(xg32[:, g, :, :], xt[:].rearrange("q u r -> q r u"))
+            xt = tw_bank([P, 2, T], F32)
+            for u in range(2):
+                for m in range(2):
+                    k0 = 256 * g + 128 * u
+                    nc.tensor.transpose(xt[:, u, m * P:(m + 1) * P], x32[:, m, k0:k0 + P], ident32[:])
+            bank[("x", e, g)] = xt
+
+        def evx(who, e, g):
+            if e < 0 or e >= E:
+                return
+            if g == 0:
+                xg[e] = sb.tile([P, 2, T, 4], BF16, name="xg", tag="xg", bufs=2, align_bytes=64)
+            evac(who, xg[e][:].bitcast(F32)[:, g, :, :], bank[("x", e, g)][:].rearrange("q u r -> q r u"))
+
+        def qx(e):
+            if e < 0 or e >= E:
+                return
             xc = sb.tile([P, 2, T], U32, name="xc", tag="xc", bufs=2, align_bytes=64)
             xs = sb.tile([P, 2, T], U8, name="xs", tag="xs", bufs=2, align_bytes=64)
             nc.vector.quantize_mx(
                 out=xc[:].rearrange("q g r -> q (g r)").bitcast(FP8X4),
                 scales=xs[:].rearrange("q g r -> q (g r)"),
-                in_=xg[:].rearrange("q g r t -> q (g r t)"),
+                in_=xg[e][:].rearrange("q g r t -> q (g r t)"),
             )
             x_q[e] = (xc, xs)
 
-        def prep_w(n, s):
-            if n >= UNITS:
+        def tw(c, b):
+            if c < 0 or c >= CHUNKS:
                 return
-            w32 = w_raw[(n, s)][:].bitcast(F32)
-            wg = sb.tile([P, 2, 512, 4], BF16, name="wg", tag="wg", bufs=3, align_bytes=64)
-            wg32 = wg[:].bitcast(F32)
-            for g in range(2):
-                for cp in range(2):
-                    wt = ps.tile([P, 2, 256], F32, name="wt", tag="tw", bufs=4)
-                    for u in range(2):
-                        for c2 in range(2):
-                            k0 = 256 * g + 128 * u
-                            nc.tensor.transpose(
-                                wt[:, u, c2 * P:(c2 + 1) * P], w32[:, 2 * cp + c2, k0:k0 + P], ident32[:]
-                            )
-                    evac(wg32[:, g, cp * 256:(cp + 1) * 256, :], wt[:].rearrange("q u r -> q r u"))
-            wc = sb.tile([P, 2, 512], U32, name="wc", tag="wc", bufs=4, align_bytes=64)
-            ws = sb.tile([P, 2, 512], U8, name="ws", tag="ws", bufs=4, align_bytes=64)
+            g, cp = divmod(b, 2)
+            w32 = w_raw[c][:].bitcast(F32)
+            wt = tw_bank([P, 2, 256], F32)
+            for u in range(2):
+                for c2 in range(2):
+                    k0 = 256 * g + 128 * u
+                    nc.tensor.transpose(wt[:, u, c2 * P:(c2 + 1) * P], w32[:, 2 * cp + c2, k0:k0 + P], ident32[:])
+            bank[("w", c, b)] = wt
+
+        def evw(who, c, b):
+            if c < 0 or c >= CHUNKS:
+                return
+            g, cp = divmod(b, 2)
+            if b == 0:
+                wg[c] = sb.tile([P, 2, 512, 4], BF16, name="wg", tag="wg", bufs=3, align_bytes=64)
+            evac(
+                who,
+                wg[c][:].bitcast(F32)[:, g, cp * 256:(cp + 1) * 256, :],
+                bank[("w", c, b)][:].rearrange("q u r -> q r u"),
+            )
+
+        def qw(c):
+            if c < 0 or c >= CHUNKS:
+                return
+            wc = sb.tile([P, 2, 512], U32, name="wc", tag="wc", bufs=6, align_bytes=64)
+            ws = sb.tile([P, 2, 512], U8, name="ws", tag="ws", bufs=6, align_bytes=64)
             nc.vector.quantize_mx(
                 out=wc[:].rearrange("q g r -> q (g r)").bitcast(FP8X4),
                 scales=ws[:].rearrange("q g r -> q (g r)"),
-                in_=wg[:].rearrange("q g r t -> q (g r t)"),
+                in_=wg[c][:].rearrange("q g r t -> q (g r t)"),
             )
-            w_q[(n, s)] = (wc, ws)
+            w_q[c] = (wc, ws)
 
-        def prep_b(e):
-            bt = sb.tile([P, 4, 512], BF16, name="bt", tag="bt", bufs=2)
-            for half in range(2):
-                bp = ps.tile([P, 2, 512], BF16, name="bp", tag="tw", bufs=4)
-                for q2 in range(2):
-                    for c in range(4):
-                        nc.tensor.transpose(
-                            bp[:, q2, c * P:(c + 1) * P], b_raw[e][:, 2 * half + q2, c, :], identb[:]
-                        )
-                evac(bt[:, 2 * half:2 * half + 2, :], bp[:], "s")
-            b_t[e] = bt
+        def tb(e, q):
+            if e < 0 or e >= E:
+                return
+            bp = tw_bank([P, 512], BF16)
+            for c in range(4):
+                nc.tensor.transpose(bp[:, c * P:(c + 1) * P], b_raw[e][:, q, c, :], identb[:])
+            bank[("b", e, q)] = bp
 
-        def prep_a(e):
-            ap_ = ps.tile([P, 2, 4, R], BF16, name="ap_", tag="tw", bufs=4)
-            for g in range(2):
-                for t4 in range(4):
-                    k0 = 512 * g + 128 * t4
-                    nc.tensor.transpose(ap_[:, g, t4, :], a_raw[:, e, k0:k0 + P], identb[:])
-            ag = sb.tile([P, 2, R, 4], BF16, name="ag", tag="ag", bufs=2, align_bytes=64)
-            evac(ag[:], ap_[:].rearrange("p g t r -> p g r t"), "s")
+        def evb(who, e, q):
+            if e < 0 or e >= E:
+                return
+            if e not in b_t:
+                b_t[e] = sb.tile([P, 4, 512], BF16, name="bt", tag="bt", bufs=2)
+            evac(who, b_t[e][:, q, :], bank[("b", e, q)][:])
+
+        def ta(e, g):
+            if e < 0 or e >= E:
+                return
+            at = tw_bank([P, 4, R], BF16)
+            for t4 in range(4):
+                k0 = 512 * g + 128 * t4
+                nc.tensor.transpose(at[:, t4, :], a_raw[:, e, k0:k0 + P], identb[:])
+            bank[("a", e, g)] = at
+
+        def eva(who, e, g):
+            if e < 0 or e >= E:
+                return
+            if g == 0:
+                ag[e] = sb.tile([P, 2, R, 4], BF16, name="ag", tag="ag", bufs=2, align_bytes=64)
+            evac(who, ag[e][:, g, :, :], bank[("a", e, g)][:].rearrange("p t r -> p r t"))
+
+        def qa(e):
+            if e < 0 or e >= E:
+                return
             ac = sb.tile([P, 2, R], U32, name="ac", tag="ac", bufs=2, align_bytes=64)
             asc = sb.tile([P, 2, R], U8, name="asc", tag="asc", bufs=2, align_bytes=64)
             nc.vector.quantize_mx(
                 out=ac[:].rearrange("q g r -> q (g r)").bitcast(FP8X4),
                 scales=asc[:].rearrange("q g r -> q (g r)"),
-                in_=ag[:].rearrange("q g r t -> q (g r t)"),
+                in_=ag[e][:].rearrange("q g r t -> q (g r t)"),
             )
             a_q[e] = (ac, asc)
 
-        d_sb = {}
-        h_sb = {}
-        h_q = {}
+        def tlow():
+            lp = tw_bank([P, E, 2, P], BF16)
+            for e in range(E):
+                for m in range(2):
+                    nc.tensor.transpose(lp[:, e, m, :], low_raw[:, e, m, :], identb[:])
+            nc.scalar.mul(out=low_t[:], in_=lp[:], mul=2.0)
 
-        def delta(n, m):
+        def dl(f, s):
+            if f < 0 or f >= PHASES:
+                return
+            n, m = divmod(f, 2)
             e, j = divmod(n, 2)
-            for s in range(2):
-                pd = ps.tile([P, 512], F32, name="pd", tag="pd", bufs=2)
-                nc.tensor.matmul(pd[:], lhsT=low_t[:, e, m, :], rhs=b_t[e][:, 2 * s + j, :], start=True, stop=True)
-                dt_ = sb.tile([P, 512], F32, name="dt_", tag="dt_", bufs=6)
-                evac(
-                    dt_[:].rearrange("t (p c) -> t p c", c=4),
-                    pd[:].rearrange("t (c p) -> t p c", c=4),
-                    "s",
-                )
-                d_sb[(n, m, s)] = dt_
+            pd = ps.tile([P, 512], F32, name="pd", tag="pd", bufs=2)
+            nc.tensor.matmul(pd[:], lhsT=low_t[:, e, m, :], rhs=b_t[e][:, 2 * s + j, :], start=True, stop=True)
+            bank[("d", f, s)] = pd
 
-        def base(n, m):
+        def evd(who, f, s):
+            if f < 0 or f >= PHASES:
+                return
+            dt_ = sb.tile([P, 512], F32, name="dt_", tag="dt_", bufs=6)
+            evac(
+                who,
+                dt_[:].rearrange("t (p c) -> t p c", c=4),
+                bank[("d", f, s)][:].rearrange("t (c p) -> t p c", c=4),
+            )
+            d_sb[(f, s)] = dt_
+
+        def mx(f, s):
+            if f < 0 or f >= PHASES:
+                return
+            n, m = divmod(f, 2)
             e, j = divmod(n, 2)
             xc, xs = x_q[e]
-            sums = []
-            for s in range(2):
-                wc, ws = w_q[(n, s)]
-                pb = ps.tile([P, 512], F32, name="pb", tag="pb", bufs=2)
-                for g in range(2):
-                    nc.tensor.matmul_mx(
-                        out=pb[:],
-                        lhsT=xc[:, g, m * P:(m + 1) * P].bitcast(FP8X4),
-                        lhsT_scale=xs[:, g, m * P:(m + 1) * P],
-                        rhs=wc[:, g, :].bitcast(FP8X4),
-                        rhs_scale=ws[:, g, :],
-                        start=(g == 0),
-                        stop=(g == 1),
-                    )
-                gu = sb.tile([P, 512], F32, name="gu", tag="gu%d" % s, bufs=2)
-                nc.vector.tensor_tensor(
-                    out=gu[:].rearrange("t (p c) -> t p c", c=4),
-                    in0=pb[:].rearrange("t (c p) -> t p c", c=4),
-                    in1=d_sb[(n, m, s)][:].rearrange("t (p c) -> t p c", c=4),
-                    op=ALU.add,
+            wc, ws = w_q[2 * n + s]
+            pb = ps.tile([P, 512], F32, name="pb", tag="pb", bufs=2)
+            for g in range(2):
+                nc.tensor.matmul_mx(
+                    out=pb[:],
+                    lhsT=xc[:, g, m * P:(m + 1) * P].bitcast(FP8X4),
+                    lhsT_scale=xs[:, g, m * P:(m + 1) * P],
+                    rhs=wc[:, g, :].bitcast(FP8X4),
+                    rhs_scale=ws[:, g, :],
+                    start=(g == 0),
+                    stop=(g == 1),
                 )
-                sums.append(gu)
-            sl = sb.tile([P, 512], F32, name="sl", tag="sl", bufs=2)
-            nc.scalar.activation(out=sl[:], in_=sums[0][:], func=ACT.Silu)
-            if m == 0:
-                h_new = sb.tile([P, 2, 512], F32, name="h_new", tag="h", bufs=3)
-                h_sb[n] = h_new
-            nc.vector.tensor_tensor(out=h_sb[n][:, m, :], in0=sums[1][:], in1=sl[:], op=ALU.mult)
+            bank[("m", f, s)] = pb
 
-        def store_h(n):
-            e, j = divmod(n, 2)
-            nc.gpsimd.dma_start(
-                out=out_0[e, :, 512 * j:512 * (j + 1)].rearrange("(p m) d -> p m d", m=2), in_=h_sb[n][:]
+        def add(f, s):
+            if f < 0 or f >= PHASES:
+                return
+            t = sb.tile([P, 512], F32, name="gu", tag="gu%d" % s, bufs=2)
+            nc.vector.tensor_tensor(
+                out=t[:].rearrange("t (p c) -> t p c", c=4),
+                in0=bank[("m", f, s)][:].rearrange("t (c p) -> t p c", c=4),
+                in1=d_sb[(f, s)][:].rearrange("t (p c) -> t p c", c=4),
+                op=ALU.add,
             )
+            gu[(f, s)] = t
 
-        def h_t(n):
+        def silu(f):
+            if f < 0 or f >= PHASES:
+                return
+            t = sb.tile([P, 512], F32, name="sl", tag="sl", bufs=2)
+            nc.scalar.activation(out=t[:], in_=gu[(f, 0)][:], func=ACT.Silu)
+            sl[f] = t
+
+        def mult(f):
+            if f < 0 or f >= PHASES:
+                return
+            n, m = divmod(f, 2)
+            if m == 0:
+                h_sb[n] = sb.tile([P, 2, 512], F32, name="h", tag="h", bufs=3)
+            nc.vector.tensor_tensor(out=h_sb[n][:, m, :], in0=gu[(f, 1)][:], in1=sl[f][:], op=ALU.mult)
+            if m == 1:
+                e, j = divmod(n, 2)
+                nc.gpsimd.dma_start(
+                    out=out_0[e, :, 512 * j:512 * (j + 1)].rearrange("(p m) d -> p m d", m=2), in_=h_sb[n][:]
+                )
+
+        def th(f):
+            if f < 0 or f >= PHASES:
+                return
+            n, m = divmod(f, 2)
+            hp = tw_bank([P, 4, P], F32)
+            for t4 in range(4):
+                nc.tensor.transpose(hp[:, t4, :], h_sb[n][:, m, t4 * P:(t4 + 1) * P], ident32[:])
+            bank[("h", f)] = hp
+
+        def evh(who, f):
+            if f < 0 or f >= PHASES:
+                return
+            n, m = divmod(f, 2)
+            if m == 0:
+                hg[n] = sb.tile([P, T, 4], BF16, name="hg", tag="hg", bufs=2, align_bytes=64)
+            evac(who, hg[n][:, m * P:(m + 1) * P, :], bank[("h", f)][:].rearrange("p t r -> p r t"))
+
+        def qh(n):
+            if n < 0 or n >= 2 * E:
+                return
             e, j = divmod(n, 2)
-            hg = sb.tile([P, T, 4], BF16, name="hg", tag="hg", bufs=2, align_bytes=64)
-            for m in range(2):
-                hp = ps.tile([P, 4, P], F32, name="hp", tag="tw", bufs=4)
-                for t4 in range(4):
-                    nc.tensor.transpose(hp[:, t4, :], h_sb[n][:, m, t4 * P:(t4 + 1) * P], ident32[:])
-                evac(hg[:, m * P:(m + 1) * P, :], hp[:].rearrange("p t r -> p r t"), "s")
             if j == 0:
                 hc_new = sb.tile([P, 2, T], U32, name="hc_new", tag="hc", bufs=2, align_bytes=64)
                 hs_new = sb.tile([P, 2, T], U8, name="hs_new", tag="hs", bufs=2, align_bytes=64)
                 h_q[e] = (hc_new, hs_new)
             hc, hs = h_q[e]
             nc.vector.quantize_mx(
-                out=hc[:, j, :].bitcast(FP8X4), scales=hs[:, j, :], in_=hg[:].rearrange("p r t -> p (r t)")
+                out=hc[:, j, :].bitcast(FP8X4), scales=hs[:, j, :], in_=hg[n][:].rearrange("p r t -> p (r t)")
             )
 
-        def low_d(e):
+        def ld(e):
+            if e < 0 or e >= E:
+                return
             hc, hs = h_q[e]
             ac, asc = a_q[e]
             pl = ps.tile([P, 2, R], F32, name="pl", tag="pd", bufs=2)
@@ -231,53 +311,81 @@ def tile_loralinearexpertswrapper_pa_kernel(tc, x, low_gu, W_gu, B_gu, A_d, out_
                         start=(g == 0),
                         stop=(g == 1),
                     )
+            bank[("l", e)] = pl
+
+        def evl(who, e):
+            if e < 0 or e >= E:
+                return
             lo = sb.tile([P, 2, R], F32, name="lo", tag="lo", bufs=2)
-            evac(lo[:], pl[:], "s")
+            evac(who, lo[:], bank[("l", e)][:])
             nc.gpsimd.dma_start(out=out_1[e].rearrange("(p m) r -> p m r", m=2), in_=lo[:])
 
+
         load_x(0)
-        load_w(0, 0)
-        load_w(0, 1)
-        low_raw = const.tile([P, E, 2, R], BF16, name="low_raw")
-        nc.sync.dma_start(out=low_raw[:], in_=low_gu.rearrange("e (p m) r -> p e m r", m=2))
+        load_w(0)
         load_b(0)
-        load_w(1, 0)
-        load_w(1, 1)
-        a_raw = const.tile([P, E, D], BF16, name="a_raw")
-        nc.sync.dma_start(out=a_raw[:], in_=A_d.rearrange("e r d -> r e d"))
-        load_w(2, 0)
-        load_w(2, 1)
-
-        prep_x(0)
-        prep_w(0, 0)
-        prep_w(0, 1)
-        lp = ps.tile([P, E, 2, P], BF16, name="lp", tag="tw", bufs=4)
-        for e in range(E):
-            for m in range(2):
-                nc.tensor.transpose(lp[:, e, m, :], low_raw[:, e, m, :], identb[:])
-        low_t = const.tile([P, E, 2, P], BF16, name="low_t")
-        nc.scalar.mul(out=low_t[:], in_=lp[:], mul=2.0)
-        prep_b(0)
-
-        for n in range(UNITS):
-            e, j = divmod(n, 2)
-            if j == 0 and e + 1 < E:
-                load_x(e + 1)
-                load_b(e + 1)
-            load_w(n + 3, 0)
-            load_w(n + 3, 1)
-            delta(n, 0)
-            prep_w(n + 1, 0)
-            base(n, 0)
-            delta(n, 1)
-            prep_w(n + 1, 1)
-            base(n, 1)
-            store_h(n)
-            if j == 0:
-                prep_a(e)
-            if j == 0 and e + 1 < E:
-                prep_x(e + 1)
-                prep_b(e + 1)
-            h_t(n)
-            if j == 1:
-                low_d(e)
+        nc.sync.dma_start(out=low_raw[:], in_=low_gu.rearrange("e (p m) r -> p e m r", m=2))
+        load_w(1)
+        for c in range(2, W_BUFS - 1):
+            load_w(c)
+        load_x(1)
+        load_b(1)
+        for f in range(-LW, PHASES + 3):
+            c = f + LW
+            k, r4 = divmod(f, 4)
+            kb, ib = divmod(f + 2, 4)
+            load_w(c + W_BUFS - 1)
+            if f == -LW:
+                nc.sync.dma_start(out=a_raw[:], in_=A_d.rearrange("e r d -> r e d"))
+            if ib == 0 and kb >= 1:
+                load_x(kb + 1)
+                load_b(kb + 1)
+            if f == -1:
+                tlow()
+            if r4 == 0:
+                qx(k)
+            if r4 == 2 and k >= 1:
+                qa(k)
+                if k == 1:
+                    qa(0)
+            tw(c, 0)
+            evw("v", c, 0)
+            tw(c, 1)
+            evw("s", c, 1)
+            qw(c - 1)
+            tb(kb, (0, 2, 1, 3)[ib])
+            evb("s", kb, (0, 2, 1, 3)[ib])
+            add(f - 1, 0)
+            add(f - 1, 1)
+            if ib < 2:
+                tx(kb, ib)
+            if ib < 2:
+                evx("s", kb, ib)
+            dl(f + 1, 0)
+            tw(c, 2)
+            evw("v", c, 2)
+            tw(c, 3)
+            evw("s", c, 3)
+            evd("s", f + 1, 0)
+            silu(f - 1)
+            if r4 < 2 and k >= 1:
+                ta(k, r4)
+                if k == 1:
+                    ta(0, r4)
+            if r4 < 2 and k >= 1:
+                eva("s", k, r4)
+                if k == 1:
+                    eva("s", 0, r4)
+            dl(f + 1, 1)
+            evd("s", f + 1, 1)
+            mult(f - 1)
+            th(f - 2)
+            evh("s", f - 2)
+            if f % 2 == 0:
+                qh((f - 4) // 2)
+            mx(f, 0)
+            mx(f, 1)
+            if r4 == 3 or f == PHASES + 2:
+                ld((f - 6) // 4)
+            if r4 == 3 or f == PHASES + 2:
+                evl("s", (f - 6) // 4)

@@ -251,16 +251,18 @@ def tile_loralinearexpertswrapper_pa_kernel(tc, x, low_gu, W_gu, B_gu, A_d, out_
             nc.scalar.activation(out=t[:], in_=gu[(f, 0)][:], func=ACT.Silu)
             sl[f] = t
 
-        def mult(f):
+        def mult(who, f):
             if f < 0 or f >= PHASES:
                 return
             n, m = divmod(f, 2)
             if m == 0:
                 h_sb[n] = sb.tile([P, 2, 512], F32, name="h", tag="h", bufs=3)
-            nc.vector.tensor_tensor(out=h_sb[n][:, m, :], in0=gu[(f, 1)][:], in1=sl[f][:], op=ALU.mult)
+            eng = nc.vector if who == "v" else nc.gpsimd
+            eng.tensor_tensor(out=h_sb[n][:, m, :], in0=gu[(f, 1)][:], in1=sl[f][:], op=ALU.mult)
             if m == 1:
                 e, j = divmod(n, 2)
-                nc.gpsimd.dma_start(
+                queue = nc.sync if n >= 5 else nc.gpsimd
+                queue.dma_start(
                     out=out_0[e, :, 512 * j:512 * (j + 1)].rearrange("(p m) d -> p m d", m=2), in_=h_sb[n][:]
                 )
 
@@ -281,17 +283,20 @@ def tile_loralinearexpertswrapper_pa_kernel(tc, x, low_gu, W_gu, B_gu, A_d, out_
                 hg[n] = sb.tile([P, T, 4], BF16, name="hg", tag="hg", bufs=2, align_bytes=64)
             evac(who, hg[n][:, m * P:(m + 1) * P, :], bank[("h", f)][:].rearrange("p t r -> p r t"))
 
-        def qh(n):
-            if n < 0 or n >= 2 * E:
+        def qh(f):
+            if f < 0 or f >= PHASES:
                 return
+            n, m = divmod(f, 2)
             e, j = divmod(n, 2)
-            if j == 0:
+            if j == 0 and m == 0:
                 hc_new = sb.tile([P, 2, T], U32, name="hc_new", tag="hc", bufs=2, align_bytes=64)
                 hs_new = sb.tile([P, 2, T], U8, name="hs_new", tag="hs", bufs=2, align_bytes=64)
                 h_q[e] = (hc_new, hs_new)
             hc, hs = h_q[e]
             nc.vector.quantize_mx(
-                out=hc[:, j, :].bitcast(FP8X4), scales=hs[:, j, :], in_=hg[n][:].rearrange("p r t -> p (r t)")
+                out=hc[:, j, m * P:(m + 1) * P].bitcast(FP8X4),
+                scales=hs[:, j, m * P:(m + 1) * P],
+                in_=hg[n][:, m * P:(m + 1) * P, :].rearrange("p r t -> p (r t)"),
             )
 
         def ld(e):
@@ -318,19 +323,23 @@ def tile_loralinearexpertswrapper_pa_kernel(tc, x, low_gu, W_gu, B_gu, A_d, out_
                 return
             lo = sb.tile([P, 2, R], F32, name="lo", tag="lo", bufs=2)
             evac(who, lo[:], bank[("l", e)][:])
-            nc.gpsimd.dma_start(out=out_1[e].rearrange("(p m) r -> p m r", m=2), in_=lo[:])
+            queue = nc.sync if e >= 2 else nc.gpsimd
+            queue.dma_start(out=out_1[e].rearrange("(p m) r -> p m r", m=2), in_=lo[:])
 
 
         load_x(0)
         load_w(0)
         load_b(0)
         nc.sync.dma_start(out=low_raw[:], in_=low_gu.rearrange("e (p m) r -> p e m r", m=2))
-        load_w(1)
-        for c in range(2, W_BUFS - 1):
+        for c in range(1, W_BUFS - 1):
             load_w(c)
         load_x(1)
         load_b(1)
-        for f in range(-LW, PHASES + 3):
+        tx(0, 0)
+        evx("v", 0, 0)
+        tx(0, 1)
+        evx("s", 0, 1)
+        for f in range(-LW, PHASES):
             c = f + LW
             k, r4 = divmod(f, 4)
             kb, ib = divmod(f + 2, 4)
@@ -342,50 +351,65 @@ def tile_loralinearexpertswrapper_pa_kernel(tc, x, low_gu, W_gu, B_gu, A_d, out_
                 load_b(kb + 1)
             if f == -1:
                 tlow()
-            if r4 == 0:
+                qx(0)
+            tw(c, 0)
+            tw(c, 1)
+            add(f - 1, 0)
+            evw("v", c, 0)
+            tw(c, 3)
+            evw("s", c, 1)
+            add(f - 1, 1)
+            if r4 == 0 and k >= 1:
                 qx(k)
             if r4 == 2 and k >= 1:
-                qa(k)
                 if k == 1:
                     qa(0)
-            tw(c, 0)
-            evw("v", c, 0)
-            tw(c, 1)
-            evw("s", c, 1)
+                qa(k)
+            evw("s", c, 3)
             qw(c - 1)
+            if r4 == 3:
+                ld(k - 1)
+            qh(f - 3)
             tb(kb, (0, 2, 1, 3)[ib])
-            evb("s", kb, (0, 2, 1, 3)[ib])
-            add(f - 1, 0)
-            add(f - 1, 1)
-            if ib < 2:
-                tx(kb, ib)
-            if ib < 2:
-                evx("s", kb, ib)
-            dl(f + 1, 0)
             tw(c, 2)
             evw("v", c, 2)
-            tw(c, 3)
-            evw("s", c, 3)
-            evd("s", f + 1, 0)
+            evb("s", kb, (0, 2, 1, 3)[ib])
+            dl(f + 1, 0)
+            th(f - 2)
             silu(f - 1)
             if r4 < 2 and k >= 1:
-                ta(k, r4)
                 if k == 1:
                     ta(0, r4)
+                ta(k, r4)
+            if ib < 2 and kb >= 1:
+                tx(kb, ib)
+            evh("s", f - 2)
             if r4 < 2 and k >= 1:
-                eva("s", k, r4)
                 if k == 1:
                     eva("s", 0, r4)
-            dl(f + 1, 1)
-            evd("s", f + 1, 1)
-            mult(f - 1)
-            th(f - 2)
-            evh("s", f - 2)
-            if f % 2 == 0:
-                qh((f - 4) // 2)
+                eva("s", k, r4)
             mx(f, 0)
             mx(f, 1)
-            if r4 == 3 or f == PHASES + 2:
-                ld((f - 6) // 4)
-            if r4 == 3 or f == PHASES + 2:
-                evl("s", (f - 6) // 4)
+            if r4 == 3:
+                evl("s", k - 1)
+            evd("s", f + 1, 0)
+            dl(f + 1, 1)
+            evd("s", f + 1, 1)
+            mult("g", f - 1)
+            if ib < 2 and kb >= 1:
+                evx("v", kb, ib)
+
+        f = PHASES
+        th(f - 2)
+        evh("s", f - 2)
+        add(f - 1, 0)
+        silu(f - 1)
+        add(f - 1, 1)
+        qh(f - 3)
+        mult("v", f - 1)
+        th(f - 1)
+        evh("s", f - 1)
+        qh(f - 2)
+        qh(f - 1)
+        ld(E - 1)
+        evl("v", E - 1)

@@ -157,27 +157,23 @@ def tile_loralinearexpertswrapper_pa_kernel(tc, x, low_gu, W_gu, B_gu, A_d, out_
                 b_t[e] = sb.tile([P, 4, 512], BF16, name="bt", tag="bt", bufs=2)
             evac(who, b_t[e][:, q, :], bank[("b", e, q)][:])
 
-        def ta(e, g):
-            if e < 0 or e >= E:
-                return
-            at = tw_bank([P, 4, R], BF16)
-            for t4 in range(4):
-                k0 = 512 * g + 128 * t4
-                nc.tensor.transpose(at[:, t4, :], a_raw[:, e, k0:k0 + P], identb[:])
-            bank[("a", e, g)] = at
+        def ta(e):
+            at = tw_bank([P, 2, 4, R], BF16)
+            for g in range(2):
+                for t4 in range(4):
+                    k0 = 512 * g + 128 * t4
+                    nc.tensor.transpose(at[:, g, t4, :], a_raw[:, e, k0:k0 + P], identb[:])
+            bank[("a", e)] = at
 
-        def eva(who, e, g):
-            if e < 0 or e >= E:
-                return
-            if g == 0:
-                ag[e] = sb.tile([P, 2, R, 4], BF16, name="ag", tag="ag", bufs=2, align_bytes=64)
-            evac(who, ag[e][:, g, :, :], bank[("a", e, g)][:].rearrange("p t r -> p r t"))
+        def eva(who, e):
+            ag[e] = sb.tile([P, 2, R, 4], BF16, name="ag", tag="ag", bufs=E, align_bytes=64)
+            evac(who, ag[e][:], bank[("a", e)][:].rearrange("p g t r -> p g r t"))
 
         def qa(e):
             if e < 0 or e >= E:
                 return
-            ac = sb.tile([P, 2, R], U32, name="ac", tag="ac", bufs=2, align_bytes=64)
-            asc = sb.tile([P, 2, R], U8, name="asc", tag="asc", bufs=2, align_bytes=64)
+            ac = sb.tile([P, 2, R], U32, name="ac", tag="ac", bufs=E, align_bytes=64)
+            asc = sb.tile([P, 2, R], U8, name="asc", tag="asc", bufs=E, align_bytes=64)
             nc.vector.quantize_mx(
                 out=ac[:].rearrange("q g r -> q (g r)").bitcast(FP8X4),
                 scales=asc[:].rearrange("q g r -> q (g r)"),
@@ -212,14 +208,17 @@ def tile_loralinearexpertswrapper_pa_kernel(tc, x, low_gu, W_gu, B_gu, A_d, out_
             )
             d_sb[(f, s)] = dt_
 
-        def mx(f, s):
+        def mx(f, s, spare=False):
             if f < 0 or f >= PHASES:
                 return
             n, m = divmod(f, 2)
             e, j = divmod(n, 2)
             xc, xs = x_q[e]
             wc, ws = w_q[2 * n + s]
-            pb = ps.tile([P, 512], F32, name="pb", tag="pb", bufs=2)
+            if spare:
+                pb = tw_bank([P, 512], F32)
+            else:
+                pb = ps.tile([P, 512], F32, name="pb", tag="pb", bufs=2)
             for g in range(2):
                 nc.tensor.matmul_mx(
                     out=pb[:],
@@ -327,89 +326,137 @@ def tile_loralinearexpertswrapper_pa_kernel(tc, x, low_gu, W_gu, B_gu, A_d, out_
             queue.dma_start(out=out_1[e].rearrange("(p m) r -> p m r", m=2), in_=lo[:])
 
 
+        for e in range(E):
+            nc.sync.dma_start(out=a_raw[:, e, :], in_=A_d[e])
         load_x(0)
         load_w(0)
         load_b(0)
         nc.sync.dma_start(out=low_raw[:], in_=low_gu.rearrange("e (p m) r -> p e m r", m=2))
-        for c in range(1, W_BUFS - 1):
+        for c in range(1, W_BUFS):
             load_w(c)
         load_x(1)
         load_b(1)
+        ta(0)
+        eva("s", 0)
+        qa(0)
+        ta(1)
+        ta(2)
         tx(0, 0)
+        ta(3)
+        eva("v", 1)
+        qa(1)
+        eva("s", 2)
         evx("v", 0, 0)
         tx(0, 1)
-        evx("s", 0, 1)
-        for f in range(-LW, PHASES):
+        tw(0, 2)
+        eva("v", 3)
+        tw(0, 0)
+        evx("v", 0, 1)
+        evw("v", 0, 0)
+        evw("s", 0, 2)
+        qx(0)
+        tlow()
+        tw(0, 1)
+        evw("v", 0, 1)
+        tb(0, 2)
+        tw(0, 3)
+        evb("s", 0, 2)
+        tb(0, 0)
+        tw(1, 0)
+        qa(3)
+        evw("v", 0, 3)
+        qw(0)
+        tw(1, 2)
+        tw(1, 3)
+        load_w(W_BUFS)
+        evb("s", 0, 0)
+        dl(0, 0)
+        evw("v", 1, 0)
+        tw(1, 1)
+        evd("v", 0, 0)
+        qa(2)
+        dl(0, 1)
+        evw("s", 1, 2)
+        evw("s", 1, 3)
+        evw("v", 1, 1)
+        evd("s", 0, 1)
+        for f in range(0, PHASES - 2):
             c = f + LW
             k, r4 = divmod(f, 4)
             kb, ib = divmod(f + 2, 4)
             load_w(c + W_BUFS - 1)
-            if f == -LW:
-                nc.sync.dma_start(out=a_raw[:], in_=A_d.rearrange("e r d -> r e d"))
             if ib == 0 and kb >= 1:
                 load_x(kb + 1)
                 load_b(kb + 1)
-            if f == -1:
-                tlow()
-                qx(0)
             tw(c, 0)
-            tw(c, 1)
             add(f - 1, 0)
-            evw("v", c, 0)
-            tw(c, 3)
-            evw("s", c, 1)
             add(f - 1, 1)
-            if r4 == 0 and k >= 1:
-                qx(k)
-            if r4 == 2 and k >= 1:
-                if k == 1:
-                    qa(0)
-                qa(k)
-            evw("s", c, 3)
-            qw(c - 1)
-            if r4 == 3:
-                ld(k - 1)
-            qh(f - 3)
+            evw("v", c, 0)
+            tw(c, 1)
+            silu(f - 1)
+            evw("s", c, 1)
+            dl(f + 1, 0)
             tb(kb, (0, 2, 1, 3)[ib])
             tw(c, 2)
-            evw("v", c, 2)
             evb("s", kb, (0, 2, 1, 3)[ib])
-            dl(f + 1, 0)
-            th(f - 2)
-            silu(f - 1)
-            if r4 < 2 and k >= 1:
-                if k == 1:
-                    ta(0, r4)
-                ta(k, r4)
+            if r4 == 3:
+                ld(k - 1)
+            if r4 == 0 and k >= 1:
+                qx(k)
             if ib < 2 and kb >= 1:
                 tx(kb, ib)
-            evh("s", f - 2)
-            if r4 < 2 and k >= 1:
-                if k == 1:
-                    eva("s", 0, r4)
-                eva("s", k, r4)
-            mx(f, 0)
-            mx(f, 1)
+            qw(c - 1)
+            tw(c, 3)
+            th(f - 2)
             if r4 == 3:
                 evl("s", k - 1)
-            evd("s", f + 1, 0)
-            dl(f + 1, 1)
-            evd("s", f + 1, 1)
+            evw("s", c, 3)
+            qh(f - 3)
             mult("g", f - 1)
+            mx(f, 0)
+            evd("s", f + 1, 0)
+            evh("s", f - 2)
             if ib < 2 and kb >= 1:
                 evx("v", kb, ib)
-
-        f = PHASES
-        th(f - 2)
-        evh("s", f - 2)
-        add(f - 1, 0)
-        silu(f - 1)
-        add(f - 1, 1)
-        qh(f - 3)
-        mult("v", f - 1)
-        th(f - 1)
-        evh("s", f - 1)
-        qh(f - 2)
-        qh(f - 1)
-        ld(E - 1)
-        evl("v", E - 1)
+            mx(f, 1)
+            dl(f + 1, 1)
+            evw("v", c, 2)
+            evd("s", f + 1, 1)
+        th(12)
+        add(13, 0)
+        qh(11)
+        dl(15, 0)
+        evd("s", 15, 0)
+        add(13, 1)
+        silu(13)
+        qw(15)
+        dl(15, 1)
+        mx(15, 0, True)
+        evd("s", 15, 1)
+        mx(14, 0)
+        ld(2)
+        add(15, 0)
+        add(14, 0)
+        mult("g", 13)
+        mx(14, 1)
+        evh("s", 12)
+        mx(15, 1, True)
+        add(14, 1)
+        qh(12)
+        silu(14)
+        silu(15)
+        evl("s", 2)
+        th(13)
+        mult("g", 14)
+        add(15, 1)
+        mult("v", 15)
+        th(14)
+        evh("v", 13)
+        qh(13)
+        evh("v", 14)
+        qh(14)
+        th(15)
+        evh("s", 15)
+        qh(15)
+        ld(3)
+        evl("v", 3)

@@ -337,48 +337,48 @@ def tile_loralinearexpertswrapper_pa_kernel(tc, x, low_gu, W_gu, B_gu, A_d, out_
         load_x(1)
         load_b(1)
         ta(0)
-        eva("s", 0)
-        qa(0)
-        ta(1)
+        eva("v", 0)
         ta(2)
-        tx(0, 0)
-        ta(3)
-        eva("v", 1)
-        qa(1)
         eva("s", 2)
-        evx("v", 0, 0)
-        tx(0, 1)
-        tw(0, 2)
-        eva("v", 3)
+        ta(3)
+        ta(1)
+        tx(0, 0)
+        eva("s", 3)
         tw(0, 0)
-        evx("v", 0, 1)
-        evw("v", 0, 0)
-        evw("s", 0, 2)
-        qx(0)
-        tlow()
+        eva("s", 1)
+        tx(0, 1)
         tw(0, 1)
-        evw("v", 0, 1)
+        evw("s", 0, 0)
+        qa(0)
+        evx("v", 0, 0)
+        evx("v", 0, 1)
         tb(0, 2)
-        tw(0, 3)
+        tw(0, 2)
+        evw("s", 0, 2)
+        tlow()
+        qx(0)
+        qa(1)
         evb("s", 0, 2)
-        tb(0, 0)
-        tw(1, 0)
-        qa(3)
-        evw("v", 0, 3)
-        qw(0)
-        tw(1, 2)
-        tw(1, 3)
-        load_w(W_BUFS)
-        evb("s", 0, 0)
-        dl(0, 0)
-        evw("v", 1, 0)
-        tw(1, 1)
-        evd("v", 0, 0)
+        evw("v", 0, 1)
         qa(2)
+        tw(0, 3)
+        evw("v", 0, 3)
+        tw(1, 3)
+        tb(0, 0)
+        evb("s", 0, 0)
+        tw(1, 1)
+        qw(0)
+        tw(1, 0)
+        evw("v", 1, 0)
         dl(0, 1)
-        evw("s", 1, 2)
+        qa(3)
+        evw("s", 1, 1)
+        dl(0, 0)
+        evd("v", 0, 0)
         evw("s", 1, 3)
-        evw("v", 1, 1)
+        tw(1, 2)
+        evw("s", 1, 2)
+        load_w(W_BUFS)
         evd("s", 0, 1)
         for f in range(0, PHASES - 2):
             c = f + LW
@@ -388,75 +388,75 @@ def tile_loralinearexpertswrapper_pa_kernel(tc, x, low_gu, W_gu, B_gu, A_d, out_
             if ib == 0 and kb >= 1:
                 load_x(kb + 1)
                 load_b(kb + 1)
-            tw(c, 0)
-            add(f - 1, 0)
-            add(f - 1, 1)
-            evw("v", c, 0)
-            tw(c, 1)
-            silu(f - 1)
-            evw("s", c, 1)
-            dl(f + 1, 0)
-            tb(kb, (0, 2, 1, 3)[ib])
-            tw(c, 2)
-            evb("s", kb, (0, 2, 1, 3)[ib])
             if r4 == 3:
                 ld(k - 1)
+            tw(c, 0)
+            add(f - 1, 0)
+            silu(f - 1)
+            tw(c, 1)
+            tb(kb, (0, 2, 1, 3)[ib])
+            add(f - 1, 1)
+            tw(c, 3)
+            evw("v", c, 0)
+            evw("s", c, 1)
+            evb("s", kb, (0, 2, 1, 3)[ib])
+            dl(f + 1, 0)
             if r4 == 0 and k >= 1:
                 qx(k)
-            if ib < 2 and kb >= 1:
-                tx(kb, ib)
-            qw(c - 1)
-            tw(c, 3)
             th(f - 2)
+            qw(c - 1)
+            tw(c, 2)
+            qh(f - 3)
             if r4 == 3:
                 evl("s", k - 1)
             evw("s", c, 3)
-            qh(f - 3)
             mult("g", f - 1)
-            mx(f, 0)
+            if ib < 2 and kb >= 1:
+                tx(kb, ib)
             evd("s", f + 1, 0)
             evh("s", f - 2)
+            dl(f + 1, 1)
+            mx(f, 0)
             if ib < 2 and kb >= 1:
                 evx("v", kb, ib)
             mx(f, 1)
-            dl(f + 1, 1)
-            evw("v", c, 2)
+            evw("s", c, 2)
             evd("s", f + 1, 1)
-        th(12)
-        add(13, 0)
-        qh(11)
+        mx(15, 0, True)
         dl(15, 0)
-        evd("s", 15, 0)
+        add(13, 0)
         add(13, 1)
+        qh(11)
+        evd("s", 15, 0)
+        th(12)
         silu(13)
         qw(15)
-        dl(15, 1)
-        mx(15, 0, True)
-        evd("s", 15, 1)
-        mx(14, 0)
         ld(2)
+        dl(15, 1)
+        mx(14, 0)
         add(15, 0)
         add(14, 0)
+        evl("s", 2)
         mult("g", 13)
-        mx(14, 1)
+        evd("s", 15, 1)
         evh("s", 12)
-        mx(15, 1, True)
+        mx(14, 1)
         add(14, 1)
         qh(12)
         silu(14)
-        silu(15)
-        evl("s", 2)
+        mx(15, 1, True)
         th(13)
         mult("g", 14)
+        silu(15)
+        th(14)
+        evh("s", 13)
         add(15, 1)
         mult("v", 15)
-        th(14)
-        evh("v", 13)
+        th(15)
         qh(13)
         evh("v", 14)
         qh(14)
-        th(15)
         evh("s", 15)
         qh(15)
         ld(3)
-        evl("v", 3)
+        evl("s", 3)

@@ -303,7 +303,7 @@ def tile_loralinearexpertswrapper_pa_kernel(tc, x, low_gu, W_gu, B_gu, A_d, out_
                 return
             hc, hs = h_q[e]
             ac, asc = a_q[e]
-            pl = ps.tile([P, 2, R], F32, name="pl", tag="pd", bufs=2)
+            pl = tw_bank([P, 2, R], F32)
             for m in range(2):
                 for g in range(2):
                     nc.tensor.matmul_mx(
@@ -337,126 +337,129 @@ def tile_loralinearexpertswrapper_pa_kernel(tc, x, low_gu, W_gu, B_gu, A_d, out_
         load_x(1)
         load_b(1)
         ta(0)
-        eva("v", 0)
-        ta(2)
-        eva("s", 2)
-        ta(3)
         ta(1)
-        tx(0, 0)
-        eva("s", 3)
-        tw(0, 0)
+        ta(3)
+        eva("s", 0)
         eva("s", 1)
-        tx(0, 1)
-        tw(0, 1)
-        evw("s", 0, 0)
-        qa(0)
-        evx("v", 0, 0)
-        evx("v", 0, 1)
-        tb(0, 2)
-        tw(0, 2)
-        evw("s", 0, 2)
-        tlow()
-        qx(0)
+        eva("s", 3)
+        tx(0, 0)
         qa(1)
+        ta(2)
+        tw(0, 2)
+        eva("v", 2)
+        evx("v", 0, 0)
+        tw(0, 0)
+        evw("s", 0, 0)
+        tx(0, 1)
+        evw("v", 0, 2)
+        evx("v", 0, 1)
+        qx(0)
+        tw(0, 1)
+        evw("s", 0, 1)
+        tb(0, 2)
         evb("s", 0, 2)
-        evw("v", 0, 1)
-        qa(2)
-        tw(0, 3)
-        evw("v", 0, 3)
-        tw(1, 3)
-        tb(0, 0)
-        evb("s", 0, 0)
-        tw(1, 1)
-        qw(0)
+        tlow()
         tw(1, 0)
-        evw("v", 1, 0)
-        dl(0, 1)
-        qa(3)
-        evw("s", 1, 1)
-        dl(0, 0)
-        evd("v", 0, 0)
-        evw("s", 1, 3)
+        tb(0, 0)
+        evb("v", 0, 0)
+        evw("s", 1, 0)
+        qa(0)
+        tb(0, 1)
         tw(1, 2)
-        evw("s", 1, 2)
-        load_w(W_BUFS)
+        tw(0, 3)
+        tw(1, 3)
+        evb("v", 0, 1)
+        dl(0, 1)
+        evw("v", 1, 2)
+        dl(0, 0)
+        evw("s", 0, 3)
+        qw(0)
+        tw(1, 1)
+        qa(3)
         evd("s", 0, 1)
+        evw("s", 1, 3)
+        qa(2)
+        evw("s", 1, 1)
+        evd("s", 0, 0)
+        load_w(W_BUFS)
         for f in range(0, PHASES - 2):
             c = f + LW
             k, r4 = divmod(f, 4)
             kb, ib = divmod(f + 2, 4)
+            kt, it = divmod(f + 3, 4)
             load_w(c + W_BUFS - 1)
             if ib == 0 and kb >= 1:
                 load_x(kb + 1)
                 load_b(kb + 1)
-            if r4 == 3:
-                ld(k - 1)
-            tw(c, 0)
             add(f - 1, 0)
-            silu(f - 1)
-            tw(c, 1)
-            tb(kb, (0, 2, 1, 3)[ib])
             add(f - 1, 1)
-            tw(c, 3)
-            evw("v", c, 0)
-            evw("s", c, 1)
-            evb("s", kb, (0, 2, 1, 3)[ib])
-            dl(f + 1, 0)
+            tw(c, 0)
+            tw(c, 1)
             if r4 == 0 and k >= 1:
                 qx(k)
+            evw("v", c, 0)
+            evw("s", c, 1)
             th(f - 2)
             qw(c - 1)
-            tw(c, 2)
-            qh(f - 3)
-            if r4 == 3:
-                evl("s", k - 1)
-            evw("s", c, 3)
-            mult("g", f - 1)
+            evh("s", f - 2)
             if ib < 2 and kb >= 1:
                 tx(kb, ib)
-            evd("s", f + 1, 0)
-            evh("s", f - 2)
-            dl(f + 1, 1)
-            mx(f, 0)
+            qh(f - 3)
+            tw(c, 3)
+            tw(c, 2)
+            silu(f - 1)
             if ib < 2 and kb >= 1:
-                evx("v", kb, ib)
+                evx("s", kb, ib)
+            dl(f + 1, 0)
+            if r4 == 3:
+                ld(k - 1)
+            mx(f, 0)
             mx(f, 1)
-            evw("s", c, 2)
+            dl(f + 1, 1)
+            tb(kt, (0, 2, 1, 3)[it])
+            evw("s", c, 3)
+            mult("g", f - 1)
+            evd("s", f + 1, 0)
+            evw("v", c, 2)
             evd("s", f + 1, 1)
-        mx(15, 0, True)
-        dl(15, 0)
+            if r4 == 3:
+                evl("v", k - 1)
+            evb("s", kt, (0, 2, 1, 3)[it])
         add(13, 0)
         add(13, 1)
-        qh(11)
-        evd("s", 15, 0)
-        th(12)
-        silu(13)
         qw(15)
-        ld(2)
-        dl(15, 1)
+        silu(13)
         mx(14, 0)
-        add(15, 0)
+        qh(11)
+        dl(15, 0)
+        mx(15, 0, True)
         add(14, 0)
-        evl("s", 2)
-        mult("g", 13)
-        evd("s", 15, 1)
-        evh("s", 12)
+        evd("s", 15, 0)
         mx(14, 1)
+        add(15, 0)
+        th(12)
         add(14, 1)
-        qh(12)
         silu(14)
-        mx(15, 1, True)
-        th(13)
         mult("g", 14)
-        silu(15)
-        th(14)
-        evh("s", 13)
+        evh("s", 12)
+        mult("v", 13)
+        dl(15, 1)
+        mx(15, 1, True)
+        evd("s", 15, 1)
+        ld(2)
+        th(13)
         add(15, 1)
+        th(14)
+        silu(15)
+        evh("s", 13)
         mult("v", 15)
         th(15)
+        evl("v", 2)
+        qh(12)
         qh(13)
-        evh("v", 14)
-        qh(14)
+        evh("s", 14)
         evh("s", 15)
+        qh(14)
         qh(15)
         ld(3)
-        evl("s", 3)
+        evl("v", 3)

@@ -8,17 +8,25 @@ BF16 = mybir.dt.bfloat16
 U32 = mybir.dt.uint32
 U8 = mybir.dt.uint8
 FP8X4 = mybir.dt.float8_e4m3fn_x4
-ACT = mybir.ActivationFunctionType
-ALU = mybir.AluOpType
+SILU = mybir.ActivationFunctionType.Silu
+ADD = mybir.AluOpType.add
+MULT = mybir.AluOpType.mult
 
 E, T, H, D, R = 4, 256, 1024, 1024, 128
 P = 128
+N = 512
+K_PASS = 512
+PAIRS_PASS = K_PASS // 2
 FLOPS = 2 * E * T * (2 * D * H + 2 * D * R + D * R)
 
-LW = 2
-W_BUFS = 6
 PHASES = 4 * E
 CHUNKS = 4 * E
+CHUNK_LEAD = 2
+CHUNK_BUFS = 6
+LOADS_END = CHUNKS - CHUNK_BUFS - CHUNK_LEAD + 1
+W_MX_BUFS = 4
+LORA_BUFS = 6
+B_ORDER = (0, 2, 1, 3)
 
 
 def tile_loralinearexpertswrapper_pa_kernel(tc, x, low_gu, W_gu, B_gu, A_d, out_0, out_1):
@@ -29,437 +37,380 @@ def tile_loralinearexpertswrapper_pa_kernel(tc, x, low_gu, W_gu, B_gu, A_d, out_
         ps = ctx.enter_context(tc.psum_pool(name="ps", bufs=2))
         ctx.enter_context(tc.manual_schedule())
 
-        ident32 = const.tile([P, P], F32, name="ident32")
-        make_identity(nc, ident32[:])
-        identb = const.tile([P, P], BF16, name="identb")
-        make_identity(nc, identb[:])
+        ident_f32 = const.tile([P, P], F32, name="ident_f32")
+        make_identity(nc, ident_f32[:])
+        ident_bf16 = const.tile([P, P], BF16, name="ident_bf16")
+        make_identity(nc, ident_bf16[:])
         low_raw = const.tile([P, E, 2, R], BF16, name="low_raw")
         low_t = const.tile([P, E, 2, P], BF16, name="low_t")
         a_raw = const.tile([P, E, D], BF16, name="a_raw")
 
-        def evac(who, out, in_):
-            if who == "v":
-                nc.vector.tensor_copy(out=out, in_=in_)
-            else:
-                nc.scalar.copy(out=out, in_=in_)
+        x_raw, w_raw, b_raw = {}, {}, {}
+        turned = {}
+        x_grouped, w_grouped, a_grouped, h_grouped = {}, {}, {}, {}
+        x_mx, w_mx, a_mx, h_mx = {}, {}, {}, {}
+        b_t = {}
+        lora_ps, base_ps, low_d_ps = {}, {}, {}
+        lora_sb, gate_up, silu_gate, h_sb = {}, {}, {}, {}
 
-        w_raw, x_raw, b_raw = {}, {}, {}
-        bank = {}
-        wg, xg, ag, hg = {}, {}, {}, {}
-        x_q, w_q, b_t, a_q, h_q = {}, {}, {}, {}, {}
-        d_sb, gu, sl, h_sb = {}, {}, {}, {}
+        def transpose_bank(shape, dtype):
+            return ps.tile(shape, dtype, name="turned", tag="turned", bufs=4)
 
-        def tw_bank(shape, dtype):
-            return ps.tile(shape, dtype, name="tw", tag="tw", bufs=4)
+        def mx_tiles(name, columns, bufs=2):
+            shape = [P, 2, columns]
+            words = sb.tile(shape, U32, name=name + "_words", tag=name + "_words", bufs=bufs, align_bytes=64)
+            scales = sb.tile(shape, U8, name=name + "_scales", tag=name + "_scales", bufs=bufs, align_bytes=64)
+            return words, scales
 
-        def load_w(c):
-            if c < 0 or c >= CHUNKS:
+        def quantise_both_passes(mx, grouped):
+            words, scales = mx
+            nc.vector.quantize_mx(
+                out=words[:].rearrange("q g y -> q (g y)").bitcast(FP8X4),
+                scales=scales[:].rearrange("q g y -> q (g y)"),
+                in_=grouped[:].rearrange("q g y t -> q (g y t)"),
+            )
+
+        def store_queue(f):
+            return nc.sync if f >= LOADS_END else nc.gpsimd
+
+        def load_chunk(c):
+            if c >= CHUNKS:
                 return
-            n, s = divmod(c, 2)
-            e, j = divmod(n, 2)
-            t = sb.tile([P, 4, H], BF16, name="w_raw", tag="w_raw", bufs=W_BUFS)
-            r0 = D * s + 512 * j
-            nc.sync.dma_start(out=t[:], in_=W_gu[e, r0:r0 + 512, :].rearrange("(p c) k -> p c k", c=4))
-            w_raw[c] = t
+            e, js = divmod(c, 4)
+            j, s = divmod(js, 2)
+            w_raw[c] = sb.tile([P, 4, H], BF16, name="w_raw", tag="w_raw", bufs=CHUNK_BUFS)
+            row = D * s + N * j
+            nc.sync.dma_start(out=w_raw[c][:], in_=W_gu[e, row:row + N, :].rearrange("(p r) k -> p r k", r=4))
 
         def load_x(e):
             if e >= E:
                 return
-            t = sb.tile([P, 2, H], BF16, name="x_raw", tag="x_raw", bufs=2)
-            nc.sync.dma_start(out=t[:], in_=x[e].rearrange("(p m) k -> p m k", m=2))
-            x_raw[e] = t
+            x_raw[e] = sb.tile([P, 2, H], BF16, name="x_raw", tag="x_raw")
+            nc.sync.dma_start(out=x_raw[e][:], in_=x[e].rearrange("(p m) k -> p m k", m=2))
 
         def load_b(e):
             if e >= E:
                 return
-            t = sb.tile([P, 4, 4, R], BF16, name="b_raw", tag="b_raw", bufs=2)
-            nc.sync.dma_start(out=t[:], in_=B_gu[e].rearrange("(q p c) r -> p q c r", p=P, c=4))
-            b_raw[e] = t
+            b_raw[e] = sb.tile([P, 4, 4, R], BF16, name="b_raw", tag="b_raw")
+            nc.sync.dma_start(out=b_raw[e][:], in_=B_gu[e].rearrange("(a p r) y -> p a r y", p=P, r=4))
 
-        def tx(e, g):
-            if e < 0 or e >= E:
-                return
-            x32 = x_raw[e][:].bitcast(F32)
-            xt = tw_bank([P, 2, T], F32)
+        def transpose_x(e, g):
+            pairs = x_raw[e][:].bitcast(F32)
+            bank = transpose_bank([P, 2, T], F32)
             for u in range(2):
                 for m in range(2):
-                    k0 = 256 * g + 128 * u
-                    nc.tensor.transpose(xt[:, u, m * P:(m + 1) * P], x32[:, m, k0:k0 + P], ident32[:])
-            bank[("x", e, g)] = xt
+                    first = PAIRS_PASS * g + P * u
+                    nc.tensor.transpose(bank[:, u, m * P:(m + 1) * P], pairs[:, m, first:first + P], ident_f32[:])
+            turned[("x", e, g)] = bank
 
-        def evx(who, e, g):
-            if e < 0 or e >= E:
-                return
+        def regroup_x(e, g):
             if g == 0:
-                xg[e] = sb.tile([P, 2, T, 4], BF16, name="xg", tag="xg", bufs=2, align_bytes=64)
-            evac(who, xg[e][:].bitcast(F32)[:, g, :, :], bank[("x", e, g)][:].rearrange("q u r -> q r u"))
-
-        def qx(e):
-            if e < 0 or e >= E:
-                return
-            xc = sb.tile([P, 2, T], U32, name="xc", tag="xc", bufs=2, align_bytes=64)
-            xs = sb.tile([P, 2, T], U8, name="xs", tag="xs", bufs=2, align_bytes=64)
-            nc.vector.quantize_mx(
-                out=xc[:].rearrange("q g r -> q (g r)").bitcast(FP8X4),
-                scales=xs[:].rearrange("q g r -> q (g r)"),
-                in_=xg[e][:].rearrange("q g r t -> q (g r t)"),
+                x_grouped[e] = sb.tile([P, 2, T, 4], BF16, name="x_grouped", tag="x_grouped", align_bytes=64)
+            nc.scalar.copy(
+                out=x_grouped[e][:].bitcast(F32)[:, g, :, :], in_=turned[("x", e, g)][:].rearrange("q u y -> q y u")
             )
-            x_q[e] = (xc, xs)
 
-        def tw(c, b):
-            if c < 0 or c >= CHUNKS:
+        def quantise_x(e):
+            x_mx[e] = mx_tiles("x", T)
+            quantise_both_passes(x_mx[e], x_grouped[e])
+
+        def transpose_chunk(c, b):
+            if c < 0:
                 return
-            g, cp = divmod(b, 2)
-            w32 = w_raw[c][:].bitcast(F32)
-            wt = tw_bank([P, 2, 256], F32)
+            g, half = divmod(b, 2)
+            pairs = w_raw[c][:].bitcast(F32)
+            bank = transpose_bank([P, 2, 2 * P], F32)
             for u in range(2):
-                for c2 in range(2):
-                    k0 = 256 * g + 128 * u
-                    nc.tensor.transpose(wt[:, u, c2 * P:(c2 + 1) * P], w32[:, 2 * cp + c2, k0:k0 + P], ident32[:])
-            bank[("w", c, b)] = wt
+                for i in range(2):
+                    first = PAIRS_PASS * g + P * u
+                    nc.tensor.transpose(
+                        bank[:, u, i * P:(i + 1) * P], pairs[:, 2 * half + i, first:first + P], ident_f32[:]
+                    )
+            turned[("w", c, b)] = bank
 
-        def evw(who, c, b):
-            if c < 0 or c >= CHUNKS:
+        def regroup_chunk(c, b):
+            if c < 0:
                 return
-            g, cp = divmod(b, 2)
+            g, half = divmod(b, 2)
             if b == 0:
-                wg[c] = sb.tile([P, 2, 512, 4], BF16, name="wg", tag="wg", bufs=3, align_bytes=64)
-            evac(
-                who,
-                wg[c][:].bitcast(F32)[:, g, cp * 256:(cp + 1) * 256, :],
-                bank[("w", c, b)][:].rearrange("q u r -> q r u"),
+                w_grouped[c] = sb.tile([P, 2, N, 4], BF16, name="w_grouped", tag="w_grouped", bufs=3, align_bytes=64)
+            copy = nc.vector.tensor_copy if b in (0, 3) else nc.scalar.copy
+            copy(
+                out=w_grouped[c][:].bitcast(F32)[:, g, half * 2 * P:(half + 1) * 2 * P, :],
+                in_=turned[("w", c, b)][:].rearrange("q u y -> q y u"),
             )
 
-        def qw(c):
-            if c < 0 or c >= CHUNKS:
+        def quantise_chunk(c):
+            if c < 0:
                 return
-            wc = sb.tile([P, 2, 512], U32, name="wc", tag="wc", bufs=6, align_bytes=64)
-            ws = sb.tile([P, 2, 512], U8, name="ws", tag="ws", bufs=6, align_bytes=64)
-            nc.vector.quantize_mx(
-                out=wc[:].rearrange("q g r -> q (g r)").bitcast(FP8X4),
-                scales=ws[:].rearrange("q g r -> q (g r)"),
-                in_=wg[c][:].rearrange("q g r t -> q (g r t)"),
-            )
-            w_q[c] = (wc, ws)
+            w_mx[c] = mx_tiles("w", N, W_MX_BUFS)
+            quantise_both_passes(w_mx[c], w_grouped[c])
 
-        def tb(e, q):
-            if e < 0 or e >= E:
+        def transpose_b(e, quarter):
+            if e >= E:
                 return
-            bp = tw_bank([P, 512], BF16)
-            for c in range(4):
-                nc.tensor.transpose(bp[:, c * P:(c + 1) * P], b_raw[e][:, q, c, :], identb[:])
-            bank[("b", e, q)] = bp
+            bank = transpose_bank([P, N], BF16)
+            for r in range(4):
+                nc.tensor.transpose(bank[:, r * P:(r + 1) * P], b_raw[e][:, quarter, r, :], ident_bf16[:])
+            turned[("b", e, quarter)] = bank
 
-        def evb(who, e, q):
-            if e < 0 or e >= E:
+        def copy_b(e, quarter):
+            if e >= E:
                 return
             if e not in b_t:
-                b_t[e] = sb.tile([P, 4, 512], BF16, name="bt", tag="bt", bufs=2)
-            evac(who, b_t[e][:, q, :], bank[("b", e, q)][:])
+                b_t[e] = sb.tile([P, 4, N], BF16, name="b_t", tag="b_t")
+            nc.scalar.copy(out=b_t[e][:, quarter, :], in_=turned[("b", e, quarter)][:])
 
-        def ta(e):
-            at = tw_bank([P, 2, 4, R], BF16)
-            for g in range(2):
-                for t4 in range(4):
-                    k0 = 512 * g + 128 * t4
-                    nc.tensor.transpose(at[:, g, t4, :], a_raw[:, e, k0:k0 + P], identb[:])
-            bank[("a", e)] = at
-
-        def eva(who, e):
-            ag[e] = sb.tile([P, 2, R, 4], BF16, name="ag", tag="ag", bufs=E, align_bytes=64)
-            evac(who, ag[e][:], bank[("a", e)][:].rearrange("p g t r -> p g r t"))
-
-        def qa(e):
-            if e < 0 or e >= E:
-                return
-            ac = sb.tile([P, 2, R], U32, name="ac", tag="ac", bufs=E, align_bytes=64)
-            asc = sb.tile([P, 2, R], U8, name="asc", tag="asc", bufs=E, align_bytes=64)
-            nc.vector.quantize_mx(
-                out=ac[:].rearrange("q g r -> q (g r)").bitcast(FP8X4),
-                scales=asc[:].rearrange("q g r -> q (g r)"),
-                in_=ag[e][:].rearrange("q g r t -> q (g r t)"),
-            )
-            a_q[e] = (ac, asc)
-
-        def tlow():
-            lp = tw_bank([P, E, 2, P], BF16)
+        def transpose_low():
+            bank = transpose_bank([P, E, 2, P], BF16)
             for e in range(E):
                 for m in range(2):
-                    nc.tensor.transpose(lp[:, e, m, :], low_raw[:, e, m, :], identb[:])
-            nc.scalar.mul(out=low_t[:], in_=lp[:], mul=2.0)
+                    nc.tensor.transpose(bank[:, e, m, :], low_raw[:, e, m, :], ident_bf16[:])
+            nc.scalar.mul(out=low_t[:], in_=bank[:], mul=2.0)
 
-        def dl(f, s):
-            if f < 0 or f >= PHASES:
-                return
-            n, m = divmod(f, 2)
-            e, j = divmod(n, 2)
-            pd = ps.tile([P, 512], F32, name="pd", tag="pd", bufs=2)
-            nc.tensor.matmul(pd[:], lhsT=low_t[:, e, m, :], rhs=b_t[e][:, 2 * s + j, :], start=True, stop=True)
-            bank[("d", f, s)] = pd
+        def transpose_a(e):
+            bank = transpose_bank([P, 2, 4, R], BF16)
+            for g in range(2):
+                for t in range(4):
+                    first = K_PASS * g + P * t
+                    nc.tensor.transpose(bank[:, g, t, :], a_raw[:, e, first:first + P], ident_bf16[:])
+            turned[("a", e)] = bank
 
-        def evd(who, f, s):
-            if f < 0 or f >= PHASES:
+        def regroup_a(e):
+            a_grouped[e] = sb.tile([P, 2, R, 4], BF16, name="a_grouped", tag="a_grouped", bufs=E, align_bytes=64)
+            copy = nc.scalar.copy if e % 2 == 0 else nc.vector.tensor_copy
+            copy(out=a_grouped[e][:], in_=turned[("a", e)][:].rearrange("q g t y -> q g y t"))
+
+        def quantise_a(e):
+            a_mx[e] = mx_tiles("a", R, E)
+            quantise_both_passes(a_mx[e], a_grouped[e])
+
+        def lora_matmul(f, s):
+            if f < 0:
                 return
-            dt_ = sb.tile([P, 512], F32, name="dt_", tag="dt_", bufs=6)
-            evac(
-                who,
-                dt_[:].rearrange("t (p c) -> t p c", c=4),
-                bank[("d", f, s)][:].rearrange("t (c p) -> t p c", c=4),
+            e, jm = divmod(f, 4)
+            j, m = divmod(jm, 2)
+            lora_ps[(f, s)] = ps.tile([P, N], F32, name="lora_ps", tag="lora_ps")
+            nc.tensor.matmul(
+                lora_ps[(f, s)][:], lhsT=low_t[:, e, m, :], rhs=b_t[e][:, 2 * s + j, :], start=True, stop=True
             )
-            d_sb[(f, s)] = dt_
 
-        def mx(f, s, spare=False):
-            if f < 0 or f >= PHASES:
+        def copy_lora(f, s):
+            if f < 0:
                 return
-            n, m = divmod(f, 2)
-            e, j = divmod(n, 2)
-            xc, xs = x_q[e]
-            wc, ws = w_q[2 * n + s]
-            if spare:
-                pb = tw_bank([P, 512], F32)
+            lora_sb[(f, s)] = sb.tile([P, N], F32, name="lora_sb", tag="lora_sb", bufs=LORA_BUFS)
+            nc.scalar.copy(
+                out=lora_sb[(f, s)][:].rearrange("z (p r) -> z p r", r=4),
+                in_=lora_ps[(f, s)][:].rearrange("z (r p) -> z p r", r=4),
+            )
+
+        def base_matmul(f, s, spare_bank=False):
+            if f < 0:
+                return
+            e, jm = divmod(f, 4)
+            m = jm % 2
+            x_words, x_scales = x_mx[e]
+            w_words, w_scales = w_mx[2 * (f // 2) + s]
+            if spare_bank:
+                base_ps[(f, s)] = transpose_bank([P, N], F32)
             else:
-                pb = ps.tile([P, 512], F32, name="pb", tag="pb", bufs=2)
+                base_ps[(f, s)] = ps.tile([P, N], F32, name="base_ps", tag="base_ps")
             for g in range(2):
                 nc.tensor.matmul_mx(
-                    out=pb[:],
-                    lhsT=xc[:, g, m * P:(m + 1) * P].bitcast(FP8X4),
-                    lhsT_scale=xs[:, g, m * P:(m + 1) * P],
-                    rhs=wc[:, g, :].bitcast(FP8X4),
-                    rhs_scale=ws[:, g, :],
+                    out=base_ps[(f, s)][:],
+                    lhsT=x_words[:, g, m * P:(m + 1) * P].bitcast(FP8X4),
+                    lhsT_scale=x_scales[:, g, m * P:(m + 1) * P],
+                    rhs=w_words[:, g, :].bitcast(FP8X4),
+                    rhs_scale=w_scales[:, g, :],
                     start=(g == 0),
                     stop=(g == 1),
                 )
-            bank[("m", f, s)] = pb
 
-        def add(f, s):
-            if f < 0 or f >= PHASES:
+        def add_lora(f, s):
+            if f < 0:
                 return
-            t = sb.tile([P, 512], F32, name="gu", tag="gu%d" % s, bufs=2)
+            gate_up[(f, s)] = sb.tile([P, N], F32, name="gate_up", tag="gate_up%d" % s)
             nc.vector.tensor_tensor(
-                out=t[:].rearrange("t (p c) -> t p c", c=4),
-                in0=bank[("m", f, s)][:].rearrange("t (c p) -> t p c", c=4),
-                in1=d_sb[(f, s)][:].rearrange("t (p c) -> t p c", c=4),
-                op=ALU.add,
+                out=gate_up[(f, s)][:].rearrange("z (p r) -> z p r", r=4),
+                in0=base_ps[(f, s)][:].rearrange("z (r p) -> z p r", r=4),
+                in1=lora_sb[(f, s)][:].rearrange("z (p r) -> z p r", r=4),
+                op=ADD,
             )
-            gu[(f, s)] = t
 
         def silu(f):
-            if f < 0 or f >= PHASES:
+            if f < 0:
                 return
-            t = sb.tile([P, 512], F32, name="sl", tag="sl", bufs=2)
-            nc.scalar.activation(out=t[:], in_=gu[(f, 0)][:], func=ACT.Silu)
-            sl[f] = t
+            silu_gate[f] = sb.tile([P, N], F32, name="silu_gate", tag="silu_gate")
+            nc.scalar.activation(out=silu_gate[f][:], in_=gate_up[(f, 0)][:], func=SILU)
 
-        def mult(who, f):
-            if f < 0 or f >= PHASES:
+        def product_and_store(f):
+            if f < 0:
                 return
-            n, m = divmod(f, 2)
+            e, jm = divmod(f, 4)
+            j, m = divmod(jm, 2)
             if m == 0:
-                h_sb[n] = sb.tile([P, 2, 512], F32, name="h", tag="h", bufs=3)
-            eng = nc.vector if who == "v" else nc.gpsimd
-            eng.tensor_tensor(out=h_sb[n][:, m, :], in0=gu[(f, 1)][:], in1=sl[f][:], op=ALU.mult)
+                h_sb[f // 2] = sb.tile([P, 2, N], F32, name="h_sb", tag="h_sb", bufs=3)
+            h_pair = h_sb[f // 2]
+            engine = nc.vector if f == PHASES - 1 else nc.gpsimd
+            engine.tensor_tensor(out=h_pair[:, m, :], in0=gate_up[(f, 1)][:], in1=silu_gate[f][:], op=MULT)
             if m == 1:
-                e, j = divmod(n, 2)
-                queue = nc.sync if n >= 5 else nc.gpsimd
-                queue.dma_start(
-                    out=out_0[e, :, 512 * j:512 * (j + 1)].rearrange("(p m) d -> p m d", m=2), in_=h_sb[n][:]
+                store_queue(f + 1).dma_start(
+                    out=out_0[e, :, N * j:N * (j + 1)].rearrange("(p m) d -> p m d", m=2), in_=h_pair[:]
                 )
 
-        def th(f):
-            if f < 0 or f >= PHASES:
+        def transpose_h(f):
+            if f < 0:
                 return
-            n, m = divmod(f, 2)
-            hp = tw_bank([P, 4, P], F32)
-            for t4 in range(4):
-                nc.tensor.transpose(hp[:, t4, :], h_sb[n][:, m, t4 * P:(t4 + 1) * P], ident32[:])
-            bank[("h", f)] = hp
+            bank = transpose_bank([P, 4, P], F32)
+            for t in range(4):
+                nc.tensor.transpose(bank[:, t, :], h_sb[f // 2][:, f % 2, t * P:(t + 1) * P], ident_f32[:])
+            turned[("h", f)] = bank
 
-        def evh(who, f):
-            if f < 0 or f >= PHASES:
+        def regroup_h(f):
+            if f < 0:
                 return
-            n, m = divmod(f, 2)
+            m = f % 2
             if m == 0:
-                hg[n] = sb.tile([P, T, 4], BF16, name="hg", tag="hg", bufs=2, align_bytes=64)
-            evac(who, hg[n][:, m * P:(m + 1) * P, :], bank[("h", f)][:].rearrange("p t r -> p r t"))
-
-        def qh(f):
-            if f < 0 or f >= PHASES:
-                return
-            n, m = divmod(f, 2)
-            e, j = divmod(n, 2)
-            if j == 0 and m == 0:
-                hc_new = sb.tile([P, 2, T], U32, name="hc_new", tag="hc", bufs=2, align_bytes=64)
-                hs_new = sb.tile([P, 2, T], U8, name="hs_new", tag="hs", bufs=2, align_bytes=64)
-                h_q[e] = (hc_new, hs_new)
-            hc, hs = h_q[e]
-            nc.vector.quantize_mx(
-                out=hc[:, j, m * P:(m + 1) * P].bitcast(FP8X4),
-                scales=hs[:, j, m * P:(m + 1) * P],
-                in_=hg[n][:, m * P:(m + 1) * P, :].rearrange("p r t -> p (r t)"),
+                h_grouped[f // 2] = sb.tile([P, T, 4], BF16, name="h_grouped", tag="h_grouped", align_bytes=64)
+            nc.scalar.copy(
+                out=h_grouped[f // 2][:, m * P:(m + 1) * P, :], in_=turned[("h", f)][:].rearrange("q t y -> q y t")
             )
 
-        def ld(e):
-            if e < 0 or e >= E:
+        def quantise_h(f):
+            if f < 0:
                 return
-            hc, hs = h_q[e]
-            ac, asc = a_q[e]
-            pl = tw_bank([P, 2, R], F32)
+            e, jm = divmod(f, 4)
+            j, m = divmod(jm, 2)
+            if jm == 0:
+                h_mx[e] = mx_tiles("h", T)
+            words, scales = h_mx[e]
+            nc.vector.quantize_mx(
+                out=words[:, j, m * P:(m + 1) * P].bitcast(FP8X4),
+                scales=scales[:, j, m * P:(m + 1) * P],
+                in_=h_grouped[f // 2][:, m * P:(m + 1) * P, :].rearrange("q y t -> q (y t)"),
+            )
+
+        def low_d_matmul(e):
+            if e < 0:
+                return
+            h_words, h_scales = h_mx[e]
+            a_words, a_scales = a_mx[e]
+            low_d_ps[e] = transpose_bank([P, 2, R], F32)
             for m in range(2):
                 for g in range(2):
                     nc.tensor.matmul_mx(
-                        out=pl[:, m, :],
-                        lhsT=hc[:, g, m * P:(m + 1) * P].bitcast(FP8X4),
-                        lhsT_scale=hs[:, g, m * P:(m + 1) * P],
-                        rhs=ac[:, g, :].bitcast(FP8X4),
-                        rhs_scale=asc[:, g, :],
+                        out=low_d_ps[e][:, m, :],
+                        lhsT=h_words[:, g, m * P:(m + 1) * P].bitcast(FP8X4),
+                        lhsT_scale=h_scales[:, g, m * P:(m + 1) * P],
+                        rhs=a_words[:, g, :].bitcast(FP8X4),
+                        rhs_scale=a_scales[:, g, :],
                         start=(g == 0),
                         stop=(g == 1),
                     )
-            bank[("l", e)] = pl
 
-        def evl(who, e):
-            if e < 0 or e >= E:
+        def store_low_d(e):
+            if e < 0:
                 return
-            lo = sb.tile([P, 2, R], F32, name="lo", tag="lo", bufs=2)
-            evac(who, lo[:], bank[("l", e)][:])
-            queue = nc.sync if e >= 2 else nc.gpsimd
-            queue.dma_start(out=out_1[e].rearrange("(p m) r -> p m r", m=2), in_=lo[:])
-
+            low_d_sb = sb.tile([P, 2, R], F32, name="low_d_sb", tag="low_d_sb")
+            nc.vector.tensor_copy(out=low_d_sb[:], in_=low_d_ps[e][:])
+            store_queue(4 * e + 7).dma_start(out=out_1[e].rearrange("(p m) y -> p m y", m=2), in_=low_d_sb[:])
 
         for e in range(E):
             nc.sync.dma_start(out=a_raw[:, e, :], in_=A_d[e])
         load_x(0)
-        load_w(0)
+        load_chunk(0)
         load_b(0)
-        nc.sync.dma_start(out=low_raw[:], in_=low_gu.rearrange("e (p m) r -> p e m r", m=2))
-        for c in range(1, W_BUFS):
-            load_w(c)
-        load_x(1)
-        load_b(1)
-        ta(0)
-        ta(1)
-        ta(3)
-        eva("s", 0)
-        eva("s", 1)
-        eva("s", 3)
-        tx(0, 0)
-        qa(1)
-        ta(2)
-        tw(0, 2)
-        eva("v", 2)
-        evx("v", 0, 0)
-        tw(0, 0)
-        evw("s", 0, 0)
-        tx(0, 1)
-        evw("v", 0, 2)
-        evx("v", 0, 1)
-        qx(0)
-        tw(0, 1)
-        evw("s", 0, 1)
-        tb(0, 2)
-        evb("s", 0, 2)
-        tlow()
-        tw(1, 0)
-        tb(0, 0)
-        evb("v", 0, 0)
-        evw("s", 1, 0)
-        qa(0)
-        tb(0, 1)
-        tw(1, 2)
-        tw(0, 3)
-        tw(1, 3)
-        evb("v", 0, 1)
-        dl(0, 1)
-        evw("v", 1, 2)
-        dl(0, 0)
-        evw("s", 0, 3)
-        qw(0)
-        tw(1, 1)
-        qa(3)
-        evd("s", 0, 1)
-        evw("s", 1, 3)
-        qa(2)
-        evw("s", 1, 1)
-        evd("s", 0, 0)
-        load_w(W_BUFS)
-        for f in range(0, PHASES - 2):
-            c = f + LW
-            k, r4 = divmod(f, 4)
-            kb, ib = divmod(f + 2, 4)
-            kt, it = divmod(f + 3, 4)
-            load_w(c + W_BUFS - 1)
-            if ib == 0 and kb >= 1:
-                load_x(kb + 1)
-                load_b(kb + 1)
-            add(f - 1, 0)
-            add(f - 1, 1)
-            tw(c, 0)
-            tw(c, 1)
-            if r4 == 0 and k >= 1:
-                qx(k)
-            evw("v", c, 0)
-            evw("s", c, 1)
-            th(f - 2)
-            qw(c - 1)
-            evh("s", f - 2)
-            if ib < 2 and kb >= 1:
-                tx(kb, ib)
-            qh(f - 3)
-            tw(c, 3)
-            tw(c, 2)
+        nc.sync.dma_start(out=low_raw[:], in_=low_gu.rearrange("e (p m) y -> p e m y", m=2))
+        for c in range(1, CHUNK_BUFS):
+            load_chunk(c)
+        for e in range(E):
+            transpose_a(e)
+            regroup_a(e)
+        for e in range(E):
+            quantise_a(e)
+
+        for f in range(-3, PHASES - 2):
+            c = f + CHUNK_LEAD
+            e, in_expert = divmod(f, 4)
+            next_e, x_step = divmod(f + 2, 4)
+            b_e, b_step = divmod(f + 3, 4)
+            if x_step == 0:
+                load_x(next_e + 1)
+                load_b(next_e + 1)
+            if c > 0:
+                load_chunk(c + CHUNK_BUFS - 1)
+            if f == -1:
+                transpose_low()
+            add_lora(f - 1, 0)
+            add_lora(f - 1, 1)
+            transpose_chunk(c, 0)
+            transpose_chunk(c, 1)
+            if in_expert == 0:
+                quantise_x(e)
+            regroup_chunk(c, 0)
+            regroup_chunk(c, 1)
+            transpose_h(f - 2)
+            quantise_chunk(c - 1)
+            regroup_h(f - 2)
+            if x_step < 2:
+                transpose_x(next_e, x_step)
+            quantise_h(f - 3)
+            transpose_chunk(c, 2)
+            transpose_chunk(c, 3)
             silu(f - 1)
-            if ib < 2 and kb >= 1:
-                evx("s", kb, ib)
-            dl(f + 1, 0)
-            if r4 == 3:
-                ld(k - 1)
-            mx(f, 0)
-            mx(f, 1)
-            dl(f + 1, 1)
-            tb(kt, (0, 2, 1, 3)[it])
-            evw("s", c, 3)
-            mult("g", f - 1)
-            evd("s", f + 1, 0)
-            evw("v", c, 2)
-            evd("s", f + 1, 1)
-            if r4 == 3:
-                evl("v", k - 1)
-            evb("s", kt, (0, 2, 1, 3)[it])
-        add(13, 0)
-        add(13, 1)
-        qw(15)
-        silu(13)
-        mx(14, 0)
-        qh(11)
-        dl(15, 0)
-        mx(15, 0, True)
-        add(14, 0)
-        evd("s", 15, 0)
-        mx(14, 1)
-        add(15, 0)
-        th(12)
-        add(14, 1)
-        silu(14)
-        mult("g", 14)
-        evh("s", 12)
-        mult("v", 13)
-        dl(15, 1)
-        mx(15, 1, True)
-        evd("s", 15, 1)
-        ld(2)
-        th(13)
-        add(15, 1)
-        th(14)
-        silu(15)
-        evh("s", 13)
-        mult("v", 15)
-        th(15)
-        evl("v", 2)
-        qh(12)
-        qh(13)
-        evh("s", 14)
-        evh("s", 15)
-        qh(14)
-        qh(15)
-        ld(3)
-        evl("v", 3)
+            if x_step < 2:
+                regroup_x(next_e, x_step)
+            lora_matmul(f + 1, 0)
+            if in_expert == 3:
+                low_d_matmul(e - 1)
+            base_matmul(f, 0)
+            base_matmul(f, 1)
+            lora_matmul(f + 1, 1)
+            transpose_b(b_e, B_ORDER[b_step])
+            regroup_chunk(c, 2)
+            product_and_store(f - 1)
+            copy_lora(f + 1, 0)
+            regroup_chunk(c, 3)
+            copy_lora(f + 1, 1)
+            if in_expert == 3:
+                store_low_d(e - 1)
+            copy_b(b_e, B_ORDER[b_step])
+
+        f = PHASES - 2
+        add_lora(f - 1, 0)
+        add_lora(f - 1, 1)
+        quantise_chunk(CHUNKS - 1)
+        silu(f - 1)
+        lora_matmul(f + 1, 0)
+        lora_matmul(f + 1, 1)
+        for s in range(2):
+            base_matmul(f, s)
+            base_matmul(f + 1, s, spare_bank=True)
+        copy_lora(f + 1, 0)
+        copy_lora(f + 1, 1)
+        quantise_h(f - 3)
+        product_and_store(f - 1)
+        add_lora(f, 0)
+        add_lora(f + 1, 0)
+        silu(f)
+        silu(f + 1)
+        add_lora(f, 1)
+        add_lora(f + 1, 1)
+        transpose_h(f - 2)
+        regroup_h(f - 2)
+        product_and_store(f)
+        product_and_store(f + 1)
+        transpose_h(f - 1)
+        regroup_h(f - 1)
+        low_d_matmul(E - 2)
+        quantise_h(f - 2)
+        quantise_h(f - 1)
+        store_low_d(E - 2)
+        transpose_h(f)
+        regroup_h(f)
+        transpose_h(f + 1)
+        regroup_h(f + 1)
+        quantise_h(f)
+        quantise_h(f + 1)
+        low_d_matmul(E - 1)
+        store_low_d(E - 1)

@@ -23,7 +23,6 @@ PHASES = 4 * E
 CHUNKS = 4 * E
 CHUNK_LEAD = 2
 CHUNK_BUFS = 6
-LOADS_END = CHUNKS - CHUNK_BUFS - CHUNK_LEAD + 1
 W_MX_BUFS = 4
 LORA_BUFS = 6
 B_ORDER = (0, 2, 1, 3)
@@ -69,9 +68,6 @@ def tile_loralinearexpertswrapper_pa_kernel(tc, x, low_gu, W_gu, B_gu, A_d, out_
                 scales=scales[:].rearrange("q g y -> q (g y)"),
                 in_=grouped[:].rearrange("q g y t -> q (g y t)"),
             )
-
-        def store_queue(f):
-            return nc.sync if f >= LOADS_END else nc.gpsimd
 
         def load_chunk(c):
             if c >= CHUNKS:
@@ -254,7 +250,7 @@ def tile_loralinearexpertswrapper_pa_kernel(tc, x, low_gu, W_gu, B_gu, A_d, out_
             engine = nc.vector if f == PHASES - 1 else nc.gpsimd
             engine.tensor_tensor(out=h_pair[:, m, :], in0=gate_up[(f, 1)][:], in1=silu_gate[f][:], op=MULT)
             if m == 1:
-                store_queue(f + 1).dma_start(
+                nc.sync.dma_start(
                     out=out_0[e, :, N * j:N * (j + 1)].rearrange("(p m) d -> p m d", m=2), in_=h_pair[:]
                 )
 
@@ -313,7 +309,7 @@ def tile_loralinearexpertswrapper_pa_kernel(tc, x, low_gu, W_gu, B_gu, A_d, out_
                 return
             low_d_sb = sb.tile([P, 2, R], F32, name="low_d_sb", tag="low_d_sb")
             nc.vector.tensor_copy(out=low_d_sb[:], in_=low_d_ps[e][:])
-            store_queue(4 * e + 7).dma_start(out=out_1[e].rearrange("(p m) y -> p m y", m=2), in_=low_d_sb[:])
+            nc.sync.dma_start(out=out_1[e].rearrange("(p m) y -> p m y", m=2), in_=low_d_sb[:])
 
         for e in range(E):
             nc.sync.dma_start(out=a_raw[:, e, :], in_=A_d[e])

@@ -25,6 +25,7 @@ CHUNK_LEAD = 2
 CHUNK_BUFS = 6
 W_MX_BUFS = 4
 LORA_BUFS = 6
+A_PHASES = (4, 8, 11, 12)
 B_ORDER = (0, 2, 1, 3)
 
 
@@ -76,13 +77,20 @@ def tile_loralinearexpertswrapper_pa_kernel(tc, x, low_gu, W_gu, B_gu, A_d, out_
             j, s = divmod(js, 2)
             w_raw[c] = sb.tile([P, 4, H], BF16, name="w_raw", tag="w_raw", bufs=CHUNK_BUFS)
             row = D * s + N * j
-            nc.sync.dma_start(out=w_raw[c][:], in_=W_gu[e, row:row + N, :].rearrange("(p r) k -> p r k", r=4))
+            rows = W_gu[e, row:row + N, :].rearrange("(p r) k -> p r k", r=4)
+            pieces = 2 if c < 2 else 1
+            size = 4 // pieces
+            for i in range(0, 4, size):
+                nc.sync.dma_start(out=w_raw[c][:, i:i + size, :], in_=rows[:, i:i + size, :])
 
         def load_x(e):
             if e >= E:
                 return
             x_raw[e] = sb.tile([P, 2, H], BF16, name="x_raw", tag="x_raw")
             nc.sync.dma_start(out=x_raw[e][:], in_=x[e].rearrange("(p m) k -> p m k", m=2))
+
+        def load_a(e):
+            nc.sync.dma_start(out=a_raw[:, e, :], in_=A_d[e])
 
         def load_b(e):
             if e >= E:
@@ -91,6 +99,8 @@ def tile_loralinearexpertswrapper_pa_kernel(tc, x, low_gu, W_gu, B_gu, A_d, out_
             nc.sync.dma_start(out=b_raw[e][:], in_=B_gu[e].rearrange("(a p r) y -> p a r y", p=P, r=4))
 
         def transpose_x(e, g):
+            if e >= E:
+                return
             pairs = x_raw[e][:].bitcast(F32)
             bank = transpose_bank([P, 2, T], F32)
             for u in range(2):
@@ -100,6 +110,8 @@ def tile_loralinearexpertswrapper_pa_kernel(tc, x, low_gu, W_gu, B_gu, A_d, out_
             turned[("x", e, g)] = bank
 
         def regroup_x(e, g):
+            if e >= E:
+                return
             if g == 0:
                 x_grouped[e] = sb.tile([P, 2, T, 4], BF16, name="x_grouped", tag="x_grouped", align_bytes=64)
             nc.scalar.copy(
@@ -107,6 +119,8 @@ def tile_loralinearexpertswrapper_pa_kernel(tc, x, low_gu, W_gu, B_gu, A_d, out_
             )
 
         def quantise_x(e):
+            if e >= E:
+                return
             x_mx[e] = mx_tiles("x", T)
             quantise_both_passes(x_mx[e], x_grouped[e])
 
@@ -128,9 +142,9 @@ def tile_loralinearexpertswrapper_pa_kernel(tc, x, low_gu, W_gu, B_gu, A_d, out_
             if c < 0:
                 return
             g, half = divmod(b, 2)
-            if b == 0:
+            if c not in w_grouped:
                 w_grouped[c] = sb.tile([P, 2, N, 4], BF16, name="w_grouped", tag="w_grouped", bufs=3, align_bytes=64)
-            copy = nc.vector.tensor_copy if b in (0, 3) else nc.scalar.copy
+            copy = nc.vector.tensor_copy if b in (1, 2) else nc.scalar.copy
             copy(
                 out=w_grouped[c][:].bitcast(F32)[:, g, half * 2 * P:(half + 1) * 2 * P, :],
                 in_=turned[("w", c, b)][:].rearrange("q u y -> q y u"),
@@ -181,14 +195,20 @@ def tile_loralinearexpertswrapper_pa_kernel(tc, x, low_gu, W_gu, B_gu, A_d, out_
             a_mx[e] = mx_tiles("a", R, E)
             quantise_both_passes(a_mx[e], a_grouped[e])
 
-        def lora_matmul(f, s):
+        def lora_matmul(f, s, half):
             if f < 0:
                 return
             e, jm = divmod(f, 4)
             j, m = divmod(jm, 2)
-            lora_ps[(f, s)] = ps.tile([P, N], F32, name="lora_ps", tag="lora_ps")
+            if half == 0:
+                lora_ps[(f, s)] = ps.tile([P, N], F32, name="lora_ps", tag="lora_ps")
+            columns = slice(half * N // 2, (half + 1) * N // 2)
             nc.tensor.matmul(
-                lora_ps[(f, s)][:], lhsT=low_t[:, e, m, :], rhs=b_t[e][:, 2 * s + j, :], start=True, stop=True
+                lora_ps[(f, s)][:, columns],
+                lhsT=low_t[:, e, m, :],
+                rhs=b_t[e][:, 2 * s + j, columns],
+                start=True,
+                stop=True,
             )
 
         def copy_lora(f, s):
@@ -311,74 +331,105 @@ def tile_loralinearexpertswrapper_pa_kernel(tc, x, low_gu, W_gu, B_gu, A_d, out_
             nc.vector.tensor_copy(out=low_d_sb[:], in_=low_d_ps[e][:])
             nc.sync.dma_start(out=out_1[e].rearrange("(p m) y -> p m y", m=2), in_=low_d_sb[:])
 
-        for e in range(E):
-            nc.sync.dma_start(out=a_raw[:, e, :], in_=A_d[e])
         load_x(0)
         load_chunk(0)
-        load_b(0)
         nc.sync.dma_start(out=low_raw[:], in_=low_gu.rearrange("e (p m) y -> p e m y", m=2))
-        for c in range(1, CHUNK_BUFS):
-            load_chunk(c)
-        for e in range(E):
-            transpose_a(e)
-            regroup_a(e)
-        for e in range(E):
-            quantise_a(e)
+        load_chunk(1)
+        load_b(0)
+        load_chunk(2)
+        load_x(1)
+        load_chunk(3)
+        load_b(1)
+        load_chunk(4)
+        load_a(0)
+        load_chunk(5)
+        load_chunk(6)
+        transpose_x(0, 0)
+        transpose_x(0, 1)
+        regroup_x(0, 0)
+        regroup_x(0, 1)
+        for b in (0, 2, 1, 3):
+            transpose_chunk(0, b)
+            regroup_chunk(0, b)
+        quantise_x(0)
+        transpose_low()
+        for b in (0, 2, 1, 3):
+            transpose_chunk(1, b)
+            regroup_chunk(1, b)
+        quantise_chunk(0)
+        for quarter in (0, 2, 1):
+            transpose_b(0, quarter)
+            copy_b(0, quarter)
+        for s in range(2):
+            lora_matmul(0, s, 0)
+            lora_matmul(0, s, 1)
+        for s in range(2):
+            copy_lora(0, s)
+        lora_matmul(1, 0, 0)
+        base_matmul(0, 0)
+        lora_matmul(1, 0, 1)
 
-        for f in range(-3, PHASES - 2):
+        for f in range(0, PHASES - 2):
             c = f + CHUNK_LEAD
             e, in_expert = divmod(f, 4)
-            next_e, x_step = divmod(f + 2, 4)
+            next_e, x_step = divmod(f + 3, 4)
             b_e, b_step = divmod(f + 3, 4)
+            if f in (2, 6, 9):
+                load_a(1 + (2, 6, 9).index(f))
             if x_step == 0:
                 load_x(next_e + 1)
                 load_b(next_e + 1)
             if c > 0:
                 load_chunk(c + CHUNK_BUFS - 1)
-            if f == -1:
-                transpose_low()
-            add_lora(f - 1, 0)
-            add_lora(f - 1, 1)
             transpose_chunk(c, 0)
             transpose_chunk(c, 1)
-            if in_expert == 0:
-                quantise_x(e)
-            regroup_chunk(c, 0)
-            regroup_chunk(c, 1)
-            transpose_h(f - 2)
             quantise_chunk(c - 1)
+            quantise_h(f - 3)
+            if in_expert == 3:
+                quantise_x(e + 1)
+            if f - 1 in A_PHASES:
+                quantise_a(A_PHASES.index(f - 1))
+            silu(f - 1)
+            regroup_chunk(c, 0)
+            if f > 0:
+                lora_matmul(f + 1, 0, 0)
+                base_matmul(f, 0)
+                lora_matmul(f + 1, 0, 1)
+            add_lora(f - 1, 1)
+            product_and_store(f - 1)
+            regroup_chunk(c, 1)
+            copy_lora(f + 1, 0)
+            transpose_h(f - 2)
             regroup_h(f - 2)
             if x_step < 2:
                 transpose_x(next_e, x_step)
-            quantise_h(f - 3)
+                regroup_x(next_e, x_step)
+            if f in A_PHASES:
+                transpose_a(A_PHASES.index(f))
+                regroup_a(A_PHASES.index(f))
             transpose_chunk(c, 2)
             transpose_chunk(c, 3)
-            silu(f - 1)
-            if x_step < 2:
-                regroup_x(next_e, x_step)
-            lora_matmul(f + 1, 0)
+            regroup_chunk(c, 2)
+            regroup_chunk(c, 3)
+            add_lora(f, 0)
+            lora_matmul(f + 1, 1, 0)
             if in_expert == 3:
                 low_d_matmul(e - 1)
-            base_matmul(f, 0)
             base_matmul(f, 1)
-            lora_matmul(f + 1, 1)
+            lora_matmul(f + 1, 1, 1)
             transpose_b(b_e, B_ORDER[b_step])
-            regroup_chunk(c, 2)
-            product_and_store(f - 1)
-            copy_lora(f + 1, 0)
-            regroup_chunk(c, 3)
             copy_lora(f + 1, 1)
             if in_expert == 3:
                 store_low_d(e - 1)
             copy_b(b_e, B_ORDER[b_step])
 
         f = PHASES - 2
-        add_lora(f - 1, 0)
-        add_lora(f - 1, 1)
         quantise_chunk(CHUNKS - 1)
         silu(f - 1)
-        lora_matmul(f + 1, 0)
-        lora_matmul(f + 1, 1)
+        add_lora(f - 1, 1)
+        for s in range(2):
+            lora_matmul(f + 1, s, 0)
+            lora_matmul(f + 1, s, 1)
         for s in range(2):
             base_matmul(f, s)
             base_matmul(f + 1, s, spare_bank=True)

@@ -24,9 +24,10 @@ CHUNKS = 4 * E
 CHUNK_LEAD = 2
 CHUNK_BUFS = 6
 W_MX_BUFS = 4
+A_BUFS = 2
+GU_BUFS = 2
+A_PHASES = (3, 7, 11, 12)
 LORA_BUFS = 6
-A_PHASES = (4, 8, 11, 12)
-B_ORDER = (0, 2, 1, 3)
 
 
 def tile_loralinearexpertswrapper_pa_kernel(tc, x, low_gu, W_gu, B_gu, A_d, out_0, out_1):
@@ -43,15 +44,14 @@ def tile_loralinearexpertswrapper_pa_kernel(tc, x, low_gu, W_gu, B_gu, A_d, out_
         make_identity(nc, ident_bf16[:])
         low_raw = const.tile([P, E, 2, R], BF16, name="low_raw")
         low_t = const.tile([P, E, 2, P], BF16, name="low_t")
-        a_raw = const.tile([P, E, D], BF16, name="a_raw")
 
-        x_raw, w_raw, b_raw = {}, {}, {}
+        x_raw, w_raw, b_raw, a_raw = {}, {}, {}, {}
         turned = {}
         x_grouped, w_grouped, a_grouped, h_grouped = {}, {}, {}, {}
         x_mx, w_mx, a_mx, h_mx = {}, {}, {}, {}
         b_t = {}
         lora_ps, base_ps, low_d_ps = {}, {}, {}
-        lora_sb, gate_up, silu_gate, h_sb = {}, {}, {}, {}
+        lora_sb, gate_up, silu_gate, h_sb, h_rounded = {}, {}, {}, {}, {}
 
         def transpose_bank(shape, dtype):
             return ps.tile(shape, dtype, name="turned", tag="turned", bufs=4)
@@ -70,7 +70,7 @@ def tile_loralinearexpertswrapper_pa_kernel(tc, x, low_gu, W_gu, B_gu, A_d, out_
                 in_=grouped[:].rearrange("q g y t -> q (g y t)"),
             )
 
-        def load_chunk(c):
+        def load_chunk(c, pieces=1):
             if c >= CHUNKS:
                 return
             e, js = divmod(c, 4)
@@ -78,10 +78,9 @@ def tile_loralinearexpertswrapper_pa_kernel(tc, x, low_gu, W_gu, B_gu, A_d, out_
             w_raw[c] = sb.tile([P, 4, H], BF16, name="w_raw", tag="w_raw", bufs=CHUNK_BUFS)
             row = D * s + N * j
             rows = W_gu[e, row:row + N, :].rearrange("(p r) k -> p r k", r=4)
-            pieces = 2 if c < 2 else 1
             size = 4 // pieces
-            for i in range(0, 4, size):
-                nc.sync.dma_start(out=w_raw[c][:, i:i + size, :], in_=rows[:, i:i + size, :])
+            for r in range(0, 4, size):
+                nc.sync.dma_start(out=w_raw[c][:, r:r + size, :], in_=rows[:, r:r + size, :])
 
         def load_x(e):
             if e >= E:
@@ -89,33 +88,43 @@ def tile_loralinearexpertswrapper_pa_kernel(tc, x, low_gu, W_gu, B_gu, A_d, out_
             x_raw[e] = sb.tile([P, 2, H], BF16, name="x_raw", tag="x_raw")
             nc.sync.dma_start(out=x_raw[e][:], in_=x[e].rearrange("(p m) k -> p m k", m=2))
 
-        def load_a(e):
-            nc.sync.dma_start(out=a_raw[:, e, :], in_=A_d[e])
-
-        def load_b(e):
+        def load_b(e, j):
             if e >= E:
                 return
-            b_raw[e] = sb.tile([P, 4, 4, R], BF16, name="b_raw", tag="b_raw")
-            nc.sync.dma_start(out=b_raw[e][:], in_=B_gu[e].rearrange("(a p r) y -> p a r y", p=P, r=4))
+            b_raw[(e, j)] = sb.tile([P, 2, 4, R], BF16, name="b_raw", tag="b_raw", bufs=4)
+            rows = B_gu[e].rearrange("(s j p r) y -> p s j r y", s=2, j=2, r=4)
+            nc.sync.dma_start(out=b_raw[(e, j)][:], in_=rows[:, :, j, :, :])
 
-        def transpose_x(e, g):
+        def load_a(e):
+            if e >= E:
+                return
+            a_raw[e] = sb.tile([P, D], BF16, name="a_raw", tag="a_raw", bufs=A_BUFS)
+            nc.sync.dma_start(out=a_raw[e][:], in_=A_d[e])
+
+        def load_low(first, last):
+            nc.sync.dma_start(
+                out=low_raw[:, first:last, :, :], in_=low_gu[first:last].rearrange("e (p m) y -> p e m y", m=2)
+            )
+
+        def transpose_x(e, m):
             if e >= E:
                 return
             pairs = x_raw[e][:].bitcast(F32)
-            bank = transpose_bank([P, 2, T], F32)
-            for u in range(2):
-                for m in range(2):
+            bank = transpose_bank([P, 2, 2, P], F32)
+            for g in range(2):
+                for u in range(2):
                     first = PAIRS_PASS * g + P * u
-                    nc.tensor.transpose(bank[:, u, m * P:(m + 1) * P], pairs[:, m, first:first + P], ident_f32[:])
-            turned[("x", e, g)] = bank
+                    nc.tensor.transpose(bank[:, g, u, :], pairs[:, m, first:first + P], ident_f32[:])
+            turned[("x", e, m)] = bank
 
-        def regroup_x(e, g):
+        def regroup_x(e, m, copy):
             if e >= E:
                 return
-            if g == 0:
+            if e not in x_grouped:
                 x_grouped[e] = sb.tile([P, 2, T, 4], BF16, name="x_grouped", tag="x_grouped", align_bytes=64)
-            nc.scalar.copy(
-                out=x_grouped[e][:].bitcast(F32)[:, g, :, :], in_=turned[("x", e, g)][:].rearrange("q u y -> q y u")
+            copy(
+                out=x_grouped[e][:].bitcast(F32)[:, :, m * P:(m + 1) * P, :],
+                in_=turned[("x", e, m)][:].rearrange("q g u y -> q g y u"),
             )
 
         def quantise_x(e):
@@ -124,79 +133,71 @@ def tile_loralinearexpertswrapper_pa_kernel(tc, x, low_gu, W_gu, B_gu, A_d, out_
             x_mx[e] = mx_tiles("x", T)
             quantise_both_passes(x_mx[e], x_grouped[e])
 
-        def transpose_chunk(c, b):
-            if c < 0:
-                return
-            g, half = divmod(b, 2)
+        def transpose_chunk(c, r):
             pairs = w_raw[c][:].bitcast(F32)
-            bank = transpose_bank([P, 2, 2 * P], F32)
-            for u in range(2):
-                for i in range(2):
+            bank = transpose_bank([P, 2, 2, P], F32)
+            for g in range(2):
+                for u in range(2):
                     first = PAIRS_PASS * g + P * u
-                    nc.tensor.transpose(
-                        bank[:, u, i * P:(i + 1) * P], pairs[:, 2 * half + i, first:first + P], ident_f32[:]
-                    )
-            turned[("w", c, b)] = bank
+                    nc.tensor.transpose(bank[:, g, u, :], pairs[:, r, first:first + P], ident_f32[:])
+            turned[("w", c, r)] = bank
 
-        def regroup_chunk(c, b):
-            if c < 0:
-                return
-            g, half = divmod(b, 2)
+        def regroup_chunk(c, r, copy):
             if c not in w_grouped:
                 w_grouped[c] = sb.tile([P, 2, N, 4], BF16, name="w_grouped", tag="w_grouped", bufs=3, align_bytes=64)
-            copy = nc.vector.tensor_copy if b in (1, 2) else nc.scalar.copy
             copy(
-                out=w_grouped[c][:].bitcast(F32)[:, g, half * 2 * P:(half + 1) * 2 * P, :],
-                in_=turned[("w", c, b)][:].rearrange("q u y -> q y u"),
+                out=w_grouped[c][:].bitcast(F32)[:, :, r * P:(r + 1) * P, :],
+                in_=turned[("w", c, r)][:].rearrange("q g u y -> q g y u"),
             )
 
         def quantise_chunk(c):
-            if c < 0:
-                return
             w_mx[c] = mx_tiles("w", N, W_MX_BUFS)
             quantise_both_passes(w_mx[c], w_grouped[c])
 
-        def transpose_b(e, quarter):
+        def transpose_b(e, j):
             if e >= E:
                 return
-            bank = transpose_bank([P, N], BF16)
-            for r in range(4):
-                nc.tensor.transpose(bank[:, r * P:(r + 1) * P], b_raw[e][:, quarter, r, :], ident_bf16[:])
-            turned[("b", e, quarter)] = bank
+            bank = transpose_bank([P, 2, N], BF16)
+            for s in range(2):
+                for r in range(4):
+                    nc.tensor.transpose(bank[:, s, r * P:(r + 1) * P], b_raw[(e, j)][:, s, r, :], ident_bf16[:])
+            turned[("b", e, j)] = bank
 
-        def copy_b(e, quarter):
+        def copy_b(e, j):
             if e >= E:
                 return
-            if e not in b_t:
-                b_t[e] = sb.tile([P, 4, N], BF16, name="b_t", tag="b_t")
-            nc.scalar.copy(out=b_t[e][:, quarter, :], in_=turned[("b", e, quarter)][:])
+            b_t[(e, j)] = sb.tile([P, 2, N], BF16, name="b_t", tag="b_t", bufs=3)
+            nc.scalar.copy(out=b_t[(e, j)][:], in_=turned[("b", e, j)][:])
 
-        def transpose_low():
-            bank = transpose_bank([P, E, 2, P], BF16)
-            for e in range(E):
+        def transpose_low(first, last):
+            bank = transpose_bank([P, last - first, 2, P], BF16)
+            for e in range(first, last):
                 for m in range(2):
-                    nc.tensor.transpose(bank[:, e, m, :], low_raw[:, e, m, :], ident_bf16[:])
-            nc.scalar.mul(out=low_t[:], in_=bank[:], mul=2.0)
+                    nc.tensor.transpose(bank[:, e - first, m, :], low_raw[:, e, m, :], ident_bf16[:])
+            turned["low"] = bank
+
+        def double_low(first, last):
+            nc.scalar.mul(out=low_t[:, first:last, :, :], in_=turned["low"][:], mul=2.0)
 
         def transpose_a(e):
-            bank = transpose_bank([P, 2, 4, R], BF16)
+            pairs = a_raw[e][:].bitcast(F32)
+            bank = transpose_bank([P, 2, 2, R], F32)
             for g in range(2):
-                for t in range(4):
-                    first = K_PASS * g + P * t
-                    nc.tensor.transpose(bank[:, g, t, :], a_raw[:, e, first:first + P], ident_bf16[:])
+                for u in range(2):
+                    first = PAIRS_PASS * g + P * u
+                    nc.tensor.transpose(bank[:, g, u, :], pairs[:, first:first + P], ident_f32[:])
             turned[("a", e)] = bank
 
-        def regroup_a(e):
-            a_grouped[e] = sb.tile([P, 2, R, 4], BF16, name="a_grouped", tag="a_grouped", bufs=E, align_bytes=64)
-            copy = nc.scalar.copy if e % 2 == 0 else nc.vector.tensor_copy
-            copy(out=a_grouped[e][:], in_=turned[("a", e)][:].rearrange("q g t y -> q g y t"))
+        def regroup_a(e, copy):
+            a_grouped[e] = sb.tile([P, 2, R, 4], BF16, name="a_grouped", tag="a_grouped", align_bytes=64)
+            copy(out=a_grouped[e][:].bitcast(F32), in_=turned[("a", e)][:].rearrange("q g u y -> q g y u"))
 
         def quantise_a(e):
             a_mx[e] = mx_tiles("a", R, E)
             quantise_both_passes(a_mx[e], a_grouped[e])
 
-        def lora_matmul(f, s, half):
-            if f < 0:
+        def lora_half(f, s, half):
+            if f >= PHASES:
                 return
             e, jm = divmod(f, 4)
             j, m = divmod(jm, 2)
@@ -206,13 +207,13 @@ def tile_loralinearexpertswrapper_pa_kernel(tc, x, low_gu, W_gu, B_gu, A_d, out_
             nc.tensor.matmul(
                 lora_ps[(f, s)][:, columns],
                 lhsT=low_t[:, e, m, :],
-                rhs=b_t[e][:, 2 * s + j, columns],
+                rhs=b_t[(e, j)][:, s, columns],
                 start=True,
                 stop=True,
             )
 
         def copy_lora(f, s):
-            if f < 0:
+            if f >= PHASES:
                 return
             lora_sb[(f, s)] = sb.tile([P, N], F32, name="lora_sb", tag="lora_sb", bufs=LORA_BUFS)
             nc.scalar.copy(
@@ -221,8 +222,6 @@ def tile_loralinearexpertswrapper_pa_kernel(tc, x, low_gu, W_gu, B_gu, A_d, out_
             )
 
         def base_matmul(f, s, spare_bank=False):
-            if f < 0:
-                return
             e, jm = divmod(f, 4)
             m = jm % 2
             x_words, x_scales = x_mx[e]
@@ -245,7 +244,7 @@ def tile_loralinearexpertswrapper_pa_kernel(tc, x, low_gu, W_gu, B_gu, A_d, out_
         def add_lora(f, s):
             if f < 0:
                 return
-            gate_up[(f, s)] = sb.tile([P, N], F32, name="gate_up", tag="gate_up%d" % s)
+            gate_up[(f, s)] = sb.tile([P, N], F32, name="gate_up", tag="gate_up%d" % s, bufs=GU_BUFS)
             nc.vector.tensor_tensor(
                 out=gate_up[(f, s)][:].rearrange("z (p r) -> z p r", r=4),
                 in0=base_ps[(f, s)][:].rearrange("z (r p) -> z p r", r=4),
@@ -256,54 +255,74 @@ def tile_loralinearexpertswrapper_pa_kernel(tc, x, low_gu, W_gu, B_gu, A_d, out_
         def silu(f):
             if f < 0:
                 return
-            silu_gate[f] = sb.tile([P, N], F32, name="silu_gate", tag="silu_gate")
+            silu_gate[f] = sb.tile([P, N], F32, name="silu_gate", tag="silu_gate", bufs=GU_BUFS)
             nc.scalar.activation(out=silu_gate[f][:], in_=gate_up[(f, 0)][:], func=SILU)
 
-        def product_and_store(f):
-            if f < 0:
-                return
-            e, jm = divmod(f, 4)
-            j, m = divmod(jm, 2)
-            if m == 0:
-                h_sb[f // 2] = sb.tile([P, 2, N], F32, name="h_sb", tag="h_sb", bufs=3)
-            h_pair = h_sb[f // 2]
-            engine = nc.vector if f == PHASES - 1 else nc.gpsimd
-            engine.tensor_tensor(out=h_pair[:, m, :], in0=gate_up[(f, 1)][:], in1=silu_gate[f][:], op=MULT)
-            if m == 1:
-                nc.sync.dma_start(
-                    out=out_0[e, :, N * j:N * (j + 1)].rearrange("(p m) d -> p m d", m=2), in_=h_pair[:]
-                )
-
-        def transpose_h(f):
-            if f < 0:
-                return
-            bank = transpose_bank([P, 4, P], F32)
-            for t in range(4):
-                nc.tensor.transpose(bank[:, t, :], h_sb[f // 2][:, f % 2, t * P:(t + 1) * P], ident_f32[:])
-            turned[("h", f)] = bank
-
-        def regroup_h(f):
+        def product(f, engine):
             if f < 0:
                 return
             m = f % 2
             if m == 0:
-                h_grouped[f // 2] = sb.tile([P, T, 4], BF16, name="h_grouped", tag="h_grouped", align_bytes=64)
-            nc.scalar.copy(
-                out=h_grouped[f // 2][:, m * P:(m + 1) * P, :], in_=turned[("h", f)][:].rearrange("q t y -> q y t")
+                h_sb[f // 2] = sb.tile([P, 2, N], F32, name="h_sb", tag="h_sb", bufs=3)
+                h_rounded[f // 2] = sb.tile([P, 2, N], BF16, name="h_rounded", tag="h_rounded", bufs=2)
+            engine.tensor_tensor(
+                out=h_sb[f // 2][:, m, :], in0=gate_up[(f, 1)][:], in1=silu_gate[f][:], op=MULT
             )
 
-        def quantise_h(f):
+        def round_h(f):
             if f < 0:
                 return
-            e, jm = divmod(f, 4)
-            j, m = divmod(jm, 2)
-            if jm == 0:
+            m = f % 2
+            nc.gpsimd.tensor_scalar(
+                out=h_rounded[f // 2][:, m, :],
+                in0=h_sb[f // 2][:, m, :],
+                scalar1=1.0,
+                scalar2=0.0,
+                op0=MULT,
+                op1=ADD,
+            )
+
+        def store_h(f):
+            if f < 0 or f % 2 == 0:
+                return
+            e, j = divmod(f // 2, 2)
+            nc.sync.dma_start(
+                out=out_0[e, :, N * j:N * (j + 1)].rearrange("(p m) d -> p m d", m=2), in_=h_sb[f // 2][:]
+            )
+
+        def transpose_h(pair, tokens=(0, 1)):
+            if pair < 0:
+                return
+            bank = transpose_bank([P, len(tokens), 2, P], F32)
+            for i, m in enumerate(tokens):
+                pairs = h_rounded[pair][:].bitcast(F32)
+                for u in range(2):
+                    nc.tensor.transpose(bank[:, i, u, :], pairs[:, m, u * P:(u + 1) * P], ident_f32[:])
+            turned[("h", pair, tokens)] = bank
+
+        def regroup_h(pair, tokens=(0, 1), copy=None):
+            if pair < 0:
+                return
+            if pair not in h_grouped:
+                h_grouped[pair] = sb.tile([P, T, 4], BF16, name="h_grouped", tag="h_grouped", align_bytes=64)
+            first, last = tokens[0] * P, (tokens[-1] + 1) * P
+            (copy or nc.scalar.copy)(
+                out=h_grouped[pair][:].bitcast(F32)[:, first:last, :].rearrange("q (m y) u -> q m y u", y=P),
+                in_=turned[("h", pair, tokens)][:].rearrange("q m u y -> q m y u"),
+            )
+
+        def quantise_h(pair, tokens=(0, 1)):
+            if pair < 0:
+                return
+            e, j = divmod(pair, 2)
+            if e not in h_mx:
                 h_mx[e] = mx_tiles("h", T)
             words, scales = h_mx[e]
+            first, last = tokens[0] * P, (tokens[-1] + 1) * P
             nc.vector.quantize_mx(
-                out=words[:, j, m * P:(m + 1) * P].bitcast(FP8X4),
-                scales=scales[:, j, m * P:(m + 1) * P],
-                in_=h_grouped[f // 2][:, m * P:(m + 1) * P, :].rearrange("q y t -> q (y t)"),
+                out=words[:, j, first:last].bitcast(FP8X4),
+                scales=scales[:, j, first:last],
+                in_=h_grouped[pair][:, first:last, :].rearrange("q y t -> q (y t)"),
             )
 
         def low_d_matmul(e):
@@ -331,133 +350,151 @@ def tile_loralinearexpertswrapper_pa_kernel(tc, x, low_gu, W_gu, B_gu, A_d, out_
             nc.vector.tensor_copy(out=low_d_sb[:], in_=low_d_ps[e][:])
             nc.sync.dma_start(out=out_1[e].rearrange("(p m) y -> p m y", m=2), in_=low_d_sb[:])
 
-        load_x(0)
-        load_chunk(0)
-        nc.sync.dma_start(out=low_raw[:], in_=low_gu.rearrange("e (p m) y -> p e m y", m=2))
-        load_chunk(1)
-        load_b(0)
-        load_chunk(2)
-        load_x(1)
-        load_chunk(3)
-        load_b(1)
-        load_chunk(4)
-        load_a(0)
-        load_chunk(5)
-        load_chunk(6)
-        transpose_x(0, 0)
-        transpose_x(0, 1)
-        regroup_x(0, 0)
-        regroup_x(0, 1)
-        for b in (0, 2, 1, 3):
-            transpose_chunk(0, b)
-            regroup_chunk(0, b)
-        quantise_x(0)
-        transpose_low()
-        for b in (0, 2, 1, 3):
-            transpose_chunk(1, b)
-            regroup_chunk(1, b)
-        quantise_chunk(0)
-        for quarter in (0, 2, 1):
-            transpose_b(0, quarter)
-            copy_b(0, quarter)
-        for s in range(2):
-            lora_matmul(0, s, 0)
-            lora_matmul(0, s, 1)
-        for s in range(2):
-            copy_lora(0, s)
-        lora_matmul(1, 0, 0)
-        base_matmul(0, 0)
-        lora_matmul(1, 0, 1)
+        on_v = nc.vector.tensor_copy
+        on_s = nc.scalar.copy
 
-        for f in range(0, PHASES - 2):
+        load_chunk(0, 2)
+        load_x(0)
+        load_low(0, 1)
+        load_b(0, 0)
+        load_chunk(1, 2)
+        load_chunk(2)
+        load_b(0, 1)
+        load_chunk(3)
+        load_x(1)
+        load_low(1, E)
+        load_b(1, 0)
+        load_chunk(4)
+        load_b(1, 1)
+        load_a(0)
+        for c in range(5, CHUNK_BUFS + 1):
+            load_chunk(c)
+        for r in range(4):
+            transpose_chunk(0, r)
+            regroup_chunk(0, r, on_v if r % 2 == 0 else on_s)
+        for m in range(2):
+            transpose_x(0, m)
+            regroup_x(0, m, on_s)
+        quantise_chunk(0)
+        quantise_x(0)
+        transpose_low(0, 1)
+        double_low(0, 1)
+        transpose_b(0, 0)
+        copy_b(0, 0)
+        for r in range(2):
+            transpose_chunk(1, r)
+            regroup_chunk(1, r, on_v if r % 2 == 0 else on_s)
+        lora_half(0, 0, 0)
+        lora_half(0, 0, 1)
+        base_matmul(0, 0)
+        lora_half(1, 0, 0)
+        lora_half(1, 0, 1)
+        copy_lora(0, 0)
+        for r in range(2, 4):
+            transpose_chunk(1, r)
+            regroup_chunk(1, r, on_v if r % 2 == 0 else on_s)
+        lora_half(0, 1, 0)
+        lora_half(0, 1, 1)
+        copy_lora(0, 1)
+
+        for f in range(PHASES - 2):
             c = f + CHUNK_LEAD
             e, in_expert = divmod(f, 4)
-            next_e, x_step = divmod(f + 3, 4)
-            b_e, b_step = divmod(f + 3, 4)
-            if f in (2, 6, 9):
-                load_a(1 + (2, 6, 9).index(f))
-            if x_step == 0:
-                load_x(next_e + 1)
-                load_b(next_e + 1)
-            if c > 0:
-                load_chunk(c + CHUNK_BUFS - 1)
+            next_e = e + 1
+            if in_expert == 0:
+                load_x(e + 2)
+            load_chunk(c + CHUNK_BUFS - 1)
+            if in_expert == 1:
+                load_b(e + 2, 0)
+                load_b(e + 2, 1)
+            if in_expert == 2:
+                load_a(e + 1)
             transpose_chunk(c, 0)
             transpose_chunk(c, 1)
-            quantise_chunk(c - 1)
-            quantise_h(f - 3)
+            add_lora(f - 1, 1)
+            if f % 2 == 0:
+                quantise_h((f - 4) // 2)
             if in_expert == 3:
                 quantise_x(e + 1)
             if f - 1 in A_PHASES:
                 quantise_a(A_PHASES.index(f - 1))
+            quantise_chunk(c - 1)
             silu(f - 1)
-            regroup_chunk(c, 0)
+            product(f - 1, nc.gpsimd)
+            round_h(f - 1)
+            store_h(f - 1)
+            regroup_chunk(c, 0, on_s)
             if f > 0:
-                lora_matmul(f + 1, 0, 0)
+                lora_half(f + 1, 0, 0)
                 base_matmul(f, 0)
-                lora_matmul(f + 1, 0, 1)
-            add_lora(f - 1, 1)
-            product_and_store(f - 1)
-            regroup_chunk(c, 1)
+                lora_half(f + 1, 0, 1)
+            regroup_chunk(c, 1, on_v)
             copy_lora(f + 1, 0)
-            transpose_h(f - 2)
-            regroup_h(f - 2)
-            if x_step < 2:
-                transpose_x(next_e, x_step)
-                regroup_x(next_e, x_step)
+            if f == 1:
+                transpose_low(1, E)
+                double_low(1, E)
+            if f % 2 == 1:
+                transpose_h((f - 3) // 2)
+                regroup_h((f - 3) // 2)
+            else:
+                b_e, b_j = divmod((f + 2) // 2, 2)
+                transpose_b(b_e, b_j)
+                copy_b(b_e, b_j)
+            if in_expert in (1, 2):
+                transpose_x(e + 1, in_expert - 1)
+                regroup_x(e + 1, in_expert - 1, on_s)
             if f in A_PHASES:
                 transpose_a(A_PHASES.index(f))
-                regroup_a(A_PHASES.index(f))
+                regroup_a(A_PHASES.index(f), on_s)
             transpose_chunk(c, 2)
             transpose_chunk(c, 3)
-            regroup_chunk(c, 2)
-            regroup_chunk(c, 3)
+            regroup_chunk(c, 2, on_v)
+            regroup_chunk(c, 3, on_s)
             add_lora(f, 0)
-            lora_matmul(f + 1, 1, 0)
-            if in_expert == 3:
+            lora_half(f + 1, 1, 0)
+            if in_expert == 2:
                 low_d_matmul(e - 1)
             base_matmul(f, 1)
-            lora_matmul(f + 1, 1, 1)
-            transpose_b(b_e, B_ORDER[b_step])
+            lora_half(f + 1, 1, 1)
             copy_lora(f + 1, 1)
-            if in_expert == 3:
+            if in_expert == 2:
                 store_low_d(e - 1)
-            copy_b(b_e, B_ORDER[b_step])
 
         f = PHASES - 2
-        quantise_chunk(CHUNKS - 1)
-        silu(f - 1)
         add_lora(f - 1, 1)
+        quantise_h((f - 4) // 2)
+        quantise_chunk(CHUNKS - 1)
         for s in range(2):
-            lora_matmul(f + 1, s, 0)
-            lora_matmul(f + 1, s, 1)
-        for s in range(2):
-            base_matmul(f, s)
-            base_matmul(f + 1, s, spare_bank=True)
-        copy_lora(f + 1, 0)
-        copy_lora(f + 1, 1)
-        quantise_h(f - 3)
-        product_and_store(f - 1)
+            lora_half(f + 1, s, 0)
+            lora_half(f + 1, s, 1)
+            copy_lora(f + 1, s)
+        base_matmul(f, 0)
+        base_matmul(f + 1, 0, spare_bank=True)
+        silu(f - 1)
+        product(f - 1, nc.gpsimd)
+        round_h(f - 1)
+        store_h(f - 1)
         add_lora(f, 0)
-        add_lora(f + 1, 0)
         silu(f)
+        add_lora(f + 1, 0)
         silu(f + 1)
+        base_matmul(f, 1)
+        base_matmul(f + 1, 1, spare_bank=True)
+        low_d_matmul(E - 2)
         add_lora(f, 1)
         add_lora(f + 1, 1)
-        transpose_h(f - 2)
-        regroup_h(f - 2)
-        product_and_store(f)
-        product_and_store(f + 1)
-        transpose_h(f - 1)
-        regroup_h(f - 1)
-        low_d_matmul(E - 2)
-        quantise_h(f - 2)
-        quantise_h(f - 1)
+        product(f, nc.vector)
+        product(f + 1, nc.vector)
+        store_h(f + 1)
+        transpose_h((f - 2) // 2)
+        regroup_h((f - 2) // 2)
+        for m in range(2):
+            nc.vector.tensor_copy(out=h_rounded[f // 2][:, m, :], in_=h_sb[f // 2][:, m, :])
+            transpose_h(f // 2, (m,))
+            regroup_h(f // 2, (m,))
         store_low_d(E - 2)
-        transpose_h(f)
-        regroup_h(f)
-        transpose_h(f + 1)
-        regroup_h(f + 1)
-        quantise_h(f)
-        quantise_h(f + 1)
+        quantise_h((f - 2) // 2)
+        for m in range(2):
+            quantise_h(f // 2, (m,))
         low_d_matmul(E - 1)
         store_low_d(E - 1)

@@ -54,7 +54,7 @@ def tile_loralinearexpertswrapper_pa_kernel(tc, x, low_gu, W_gu, B_gu, A_d, out_
         lora_sb, gate_up, silu_gate, h_sb, h_rounded = {}, {}, {}, {}, {}
 
         def transpose_bank(shape, dtype):
-            return ps.tile(shape, dtype, name="turned", tag="turned", bufs=4)
+            return ps.tile(shape, dtype, name="bank", tag="bank", bufs=8)
 
         def mx_tiles(name, columns, bufs=2):
             shape = [P, 2, columns]
@@ -202,7 +202,7 @@ def tile_loralinearexpertswrapper_pa_kernel(tc, x, low_gu, W_gu, B_gu, A_d, out_
             e, jm = divmod(f, 4)
             j, m = divmod(jm, 2)
             if half == 0:
-                lora_ps[(f, s)] = ps.tile([P, N], F32, name="lora_ps", tag="lora_ps")
+                lora_ps[(f, s)] = ps.tile([P, N], F32, name="lora_ps", tag="bank", bufs=8)
             columns = slice(half * N // 2, (half + 1) * N // 2)
             nc.tensor.matmul(
                 lora_ps[(f, s)][:, columns],
@@ -229,7 +229,7 @@ def tile_loralinearexpertswrapper_pa_kernel(tc, x, low_gu, W_gu, B_gu, A_d, out_
             if spare_bank:
                 base_ps[(f, s)] = transpose_bank([P, N], F32)
             else:
-                base_ps[(f, s)] = ps.tile([P, N], F32, name="base_ps", tag="base_ps")
+                base_ps[(f, s)] = ps.tile([P, N], F32, name="base_ps", tag="bank", bufs=8)
             for g in range(2):
                 nc.tensor.matmul_mx(
                     out=base_ps[(f, s)][:],

@@ -24,8 +24,8 @@ CHUNKS = 4 * E
 CHUNK_LEAD = 2
 CHUNK_BUFS = 6
 W_MX_BUFS = 4
-A_BUFS = 2
-GU_BUFS = 2
+A_BUFS = 3
+GU_BUFS = 3
 A_PHASES = (3, 7, 11, 12)
 LORA_BUFS = 6
 
@@ -263,7 +263,7 @@ def tile_loralinearexpertswrapper_pa_kernel(tc, x, low_gu, W_gu, B_gu, A_d, out_
                 return
             m = f % 2
             if m == 0:
-                h_sb[f // 2] = sb.tile([P, 2, N], F32, name="h_sb", tag="h_sb", bufs=3)
+                h_sb[f // 2] = sb.tile([P, 2, N], F32, name="h_sb", tag="h_sb", bufs=5)
                 h_rounded[f // 2] = sb.tile([P, 2, N], BF16, name="h_rounded", tag="h_rounded", bufs=2)
             engine.tensor_tensor(
                 out=h_sb[f // 2][:, m, :], in0=gate_up[(f, 1)][:], in1=silu_gate[f][:], op=MULT
@@ -362,9 +362,9 @@ def tile_loralinearexpertswrapper_pa_kernel(tc, x, low_gu, W_gu, B_gu, A_d, out_
         load_b(0, 1)
         load_chunk(3)
         load_x(1)
-        load_low(1, E)
-        load_b(1, 0)
         load_chunk(4)
+        load_b(1, 0)
+        load_low(1, E)
         load_b(1, 1)
         load_a(0)
         for c in range(5, CHUNK_BUFS + 1):
@@ -374,14 +374,15 @@ def tile_loralinearexpertswrapper_pa_kernel(tc, x, low_gu, W_gu, B_gu, A_d, out_
             regroup_chunk(0, r, on_v if r % 2 == 0 else on_s)
         for m in range(2):
             transpose_x(0, m)
-            regroup_x(0, m, on_s)
         quantise_chunk(0)
-        quantise_x(0)
+        regroup_x(0, 0, on_s)
+        regroup_x(0, 1, on_s)
         transpose_low(0, 1)
         double_low(0, 1)
         transpose_b(0, 0)
         copy_b(0, 0)
-        for r in range(2):
+        quantise_x(0)
+        for r in range(4):
             transpose_chunk(1, r)
             regroup_chunk(1, r, on_v if r % 2 == 0 else on_s)
         lora_half(0, 0, 0)
@@ -390,12 +391,11 @@ def tile_loralinearexpertswrapper_pa_kernel(tc, x, low_gu, W_gu, B_gu, A_d, out_
         lora_half(1, 0, 0)
         lora_half(1, 0, 1)
         copy_lora(0, 0)
-        for r in range(2, 4):
-            transpose_chunk(1, r)
-            regroup_chunk(1, r, on_v if r % 2 == 0 else on_s)
         lora_half(0, 1, 0)
         lora_half(0, 1, 1)
         copy_lora(0, 1)
+        quantise_chunk(1)
+        add_lora(0, 0)
 
         for f in range(PHASES - 2):
             c = f + CHUNK_LEAD
@@ -403,12 +403,12 @@ def tile_loralinearexpertswrapper_pa_kernel(tc, x, low_gu, W_gu, B_gu, A_d, out_
             next_e = e + 1
             if in_expert == 0:
                 load_x(e + 2)
-            load_chunk(c + CHUNK_BUFS - 1)
             if in_expert == 1:
                 load_b(e + 2, 0)
                 load_b(e + 2, 1)
-            if in_expert == 2:
-                load_a(e + 1)
+            if f in (2, 6, 7):
+                load_a(1 + (2, 6, 7).index(f))
+            load_chunk(c + CHUNK_BUFS - 1)
             transpose_chunk(c, 0)
             transpose_chunk(c, 1)
             add_lora(f - 1, 1)
@@ -418,11 +418,12 @@ def tile_loralinearexpertswrapper_pa_kernel(tc, x, low_gu, W_gu, B_gu, A_d, out_
                 quantise_x(e + 1)
             if f - 1 in A_PHASES:
                 quantise_a(A_PHASES.index(f - 1))
-            quantise_chunk(c - 1)
+            if f > 0:
+                quantise_chunk(c - 1)
             silu(f - 1)
             product(f - 1, nc.gpsimd)
             round_h(f - 1)
-            store_h(f - 1)
+            store_h(f - 5)
             regroup_chunk(c, 0, on_s)
             if f > 0:
                 lora_half(f + 1, 0, 0)
@@ -430,7 +431,7 @@ def tile_loralinearexpertswrapper_pa_kernel(tc, x, low_gu, W_gu, B_gu, A_d, out_
                 lora_half(f + 1, 0, 1)
             regroup_chunk(c, 1, on_v)
             copy_lora(f + 1, 0)
-            if f == 1:
+            if f == 2:
                 transpose_low(1, E)
                 double_low(1, E)
             if f % 2 == 1:
@@ -450,7 +451,8 @@ def tile_loralinearexpertswrapper_pa_kernel(tc, x, low_gu, W_gu, B_gu, A_d, out_
             transpose_chunk(c, 3)
             regroup_chunk(c, 2, on_v)
             regroup_chunk(c, 3, on_s)
-            add_lora(f, 0)
+            if f > 0:
+                add_lora(f, 0)
             lora_half(f + 1, 1, 0)
             if in_expert == 2:
                 low_d_matmul(e - 1)
@@ -473,7 +475,8 @@ def tile_loralinearexpertswrapper_pa_kernel(tc, x, low_gu, W_gu, B_gu, A_d, out_
         silu(f - 1)
         product(f - 1, nc.gpsimd)
         round_h(f - 1)
-        store_h(f - 1)
+        for t in (5, 3, 1):
+            store_h(f - t)
         add_lora(f, 0)
         silu(f)
         add_lora(f + 1, 0)

@@ -70,6 +70,14 @@ def tile_loralinearexpertswrapper_pa_kernel(tc, x, low_gu, W_gu, B_gu, A_d, out_
                 in_=grouped[:].rearrange("q g y t -> q (g y t)"),
             )
 
+        zeros = const.tile([P, N], BF16, name="zeros")
+        nc.vector.memset(zeros[:], 0.0)
+
+        def warm_up(n):
+            for i in range(n):
+                idle_ps = transpose_bank([P, N], F32)
+                nc.tensor.matmul(idle_ps[:], lhsT=zeros[:, :P], rhs=zeros[:], start=True, stop=True)
+
         def load_chunk(c, pieces=1):
             if c >= CHUNKS:
                 return
@@ -247,8 +255,8 @@ def tile_loralinearexpertswrapper_pa_kernel(tc, x, low_gu, W_gu, B_gu, A_d, out_
             gate_up[(f, s)] = sb.tile([P, N], F32, name="gate_up", tag="gate_up%d" % s, bufs=GU_BUFS)
             nc.vector.tensor_tensor(
                 out=gate_up[(f, s)][:].rearrange("z (p r) -> z p r", r=4),
-                in0=base_ps[(f, s)][:].rearrange("z (r p) -> z p r", r=4),
-                in1=lora_sb[(f, s)][:].rearrange("z (p r) -> z p r", r=4),
+                in0=lora_sb[(f, s)][:].rearrange("z (p r) -> z p r", r=4),
+                in1=base_ps[(f, s)][:].rearrange("z (r p) -> z p r", r=4),
                 op=ADD,
             )
 
@@ -369,22 +377,29 @@ def tile_loralinearexpertswrapper_pa_kernel(tc, x, low_gu, W_gu, B_gu, A_d, out_
         load_a(0)
         for c in range(5, CHUNK_BUFS + 1):
             load_chunk(c)
+        warm_up(5)
         for r in range(4):
             transpose_chunk(0, r)
             regroup_chunk(0, r, on_v if r % 2 == 0 else on_s)
+            if r % 2 == 1:
+                warm_up(1)
         for m in range(2):
             transpose_x(0, m)
+        warm_up(1)
         quantise_chunk(0)
         regroup_x(0, 0, on_s)
         regroup_x(0, 1, on_s)
         transpose_low(0, 1)
         double_low(0, 1)
         transpose_b(0, 0)
+        warm_up(1)
         copy_b(0, 0)
         quantise_x(0)
         for r in range(4):
             transpose_chunk(1, r)
             regroup_chunk(1, r, on_v if r % 2 == 0 else on_s)
+            if r == 1:
+                warm_up(1)
         lora_half(0, 0, 0)
         lora_half(0, 0, 1)
         base_matmul(0, 0)

@@ -266,13 +266,25 @@ def tile_loralinearexpertswrapper_pa_kernel(tc, x, low_gu, W_gu, B_gu, A_d, out_
             silu_gate[f] = sb.tile([P, N], F32, name="silu_gate", tag="silu_gate", bufs=GU_BUFS)
             nc.scalar.activation(out=silu_gate[f][:], in_=gate_up[(f, 0)][:], func=SILU)
 
+        def h_rounded_tile(f):
+            t, m = divmod(f, 2)
+            if t not in h_sb:
+                h_sb[t] = sb.tile([P, 2, N], F32, name="h_sb", tag="h_sb", bufs=5)
+                h_rounded[t] = sb.tile([P, 2, N], BF16, name="h_rounded", tag="h_rounded", bufs=2)
+            return h_rounded[t][:, m, :]
+
+        def store_h_half(f):
+            t, m = divmod(f, 2)
+            e, j = divmod(t, 2)
+            nc.sync.dma_start(
+                out=out_0[e, :, N * j:N * (j + 1)].rearrange("(p m) d -> m p d", m=2)[m], in_=h_sb[t][:, m, :]
+            )
+
         def product(f, engine):
             if f < 0:
                 return
             m = f % 2
-            if m == 0:
-                h_sb[f // 2] = sb.tile([P, 2, N], F32, name="h_sb", tag="h_sb", bufs=5)
-                h_rounded[f // 2] = sb.tile([P, 2, N], BF16, name="h_rounded", tag="h_rounded", bufs=2)
+            h_rounded_tile(f)
             engine.tensor_tensor(
                 out=h_sb[f // 2][:, m, :], in0=gate_up[(f, 1)][:], in1=silu_gate[f][:], op=MULT
             )
@@ -355,7 +367,8 @@ def tile_loralinearexpertswrapper_pa_kernel(tc, x, low_gu, W_gu, B_gu, A_d, out_
             if e < 0:
                 return
             low_d_sb = sb.tile([P, 2, R], F32, name="low_d_sb", tag="low_d_sb")
-            nc.vector.tensor_copy(out=low_d_sb[:], in_=low_d_ps[e][:])
+            copy = on_s if e == E - 1 else on_v
+            copy(out=low_d_sb[:], in_=low_d_ps[e][:])
             nc.sync.dma_start(out=out_1[e].rearrange("(p m) y -> p m y", m=2), in_=low_d_sb[:])
 
         on_v = nc.vector.tensor_copy
@@ -464,10 +477,10 @@ def tile_loralinearexpertswrapper_pa_kernel(tc, x, low_gu, W_gu, B_gu, A_d, out_
                 regroup_a(A_PHASES.index(f), on_s)
             transpose_chunk(c, 2)
             transpose_chunk(c, 3)
-            regroup_chunk(c, 2, on_v)
-            regroup_chunk(c, 3, on_s)
             if f > 0:
                 add_lora(f, 0)
+            regroup_chunk(c, 2, on_v)
+            regroup_chunk(c, 3, on_s)
             lora_half(f + 1, 1, 0)
             if in_expert == 2:
                 low_d_matmul(e - 1)
@@ -481,13 +494,13 @@ def tile_loralinearexpertswrapper_pa_kernel(tc, x, low_gu, W_gu, B_gu, A_d, out_
         add_lora(f - 1, 1)
         quantise_h((f - 4) // 2)
         quantise_chunk(CHUNKS - 1)
+        silu(f - 1)
         for s in range(2):
             lora_half(f + 1, s, 0)
             lora_half(f + 1, s, 1)
             copy_lora(f + 1, s)
         base_matmul(f, 0)
         base_matmul(f + 1, 0, spare_bank=True)
-        silu(f - 1)
         product(f - 1, nc.gpsimd)
         round_h(f - 1)
         for t in (5, 3, 1):
@@ -501,18 +514,22 @@ def tile_loralinearexpertswrapper_pa_kernel(tc, x, low_gu, W_gu, B_gu, A_d, out_
         low_d_matmul(E - 2)
         add_lora(f, 1)
         add_lora(f + 1, 1)
+        for m in range(2):
+            nc.vector.tensor_tensor(
+                out=h_rounded_tile(f + m), in0=gate_up[(f + m, 1)][:], in1=silu_gate[f + m][:], op=MULT
+            )
         product(f, nc.vector)
-        product(f + 1, nc.vector)
-        store_h(f + 1)
+        store_h_half(f)
         transpose_h((f - 2) // 2)
         regroup_h((f - 2) // 2)
         for m in range(2):
-            nc.vector.tensor_copy(out=h_rounded[f // 2][:, m, :], in_=h_sb[f // 2][:, m, :])
             transpose_h(f // 2, (m,))
             regroup_h(f // 2, (m,))
         store_low_d(E - 2)
         quantise_h((f - 2) // 2)
         for m in range(2):
             quantise_h(f // 2, (m,))
+        product(f + 1, nc.vector)
+        store_h_half(f + 1)
         low_d_matmul(E - 1)
         store_low_d(E - 1)

from contextlib import ExitStack

import concourse.mybir as mybir
from concourse.masks import make_identity

F32 = mybir.dt.float32
BF16 = mybir.dt.bfloat16
U32 = mybir.dt.uint32
U8 = mybir.dt.uint8
FP8X4 = mybir.dt.float8_e4m3fn_x4
SILU = mybir.ActivationFunctionType.Silu
ADD = mybir.AluOpType.add
MULT = mybir.AluOpType.mult

E, T, H, D, R = 4, 256, 1024, 1024, 128
P = 128
N = 512
K_PASS = 512
PAIRS_PASS = K_PASS // 2
FLOPS = 2 * E * T * (2 * D * H + 2 * D * R + D * R)

PHASES = 4 * E
CHUNKS = 4 * E
CHUNK_LEAD = 2
CHUNK_BUFS = 6
W_MX_BUFS = 4
A_BUFS = 3
GU_BUFS = 3
A_PHASES = (3, 7, 11, 12)
LORA_BUFS = 6


def tile_loralinearexpertswrapper_pa_kernel(tc, x, low_gu, W_gu, B_gu, A_d, out_0, out_1):
    nc = tc.nc
    with ExitStack() as ctx:
        const = ctx.enter_context(tc.tile_pool(name="const", bufs=1))
        sb = ctx.enter_context(tc.tile_pool(name="sb", bufs=2))
        ps = ctx.enter_context(tc.psum_pool(name="ps", bufs=2))
        ctx.enter_context(tc.manual_schedule())

        ident_f32 = const.tile([P, P], F32, name="ident_f32")
        make_identity(nc, ident_f32[:])
        ident_bf16 = const.tile([P, P], BF16, name="ident_bf16")
        make_identity(nc, ident_bf16[:])
        low_raw = const.tile([P, E, 2, R], BF16, name="low_raw")
        low_t = const.tile([P, E, 2, P], BF16, name="low_t")

        x_raw, w_raw, b_raw, a_raw = {}, {}, {}, {}
        turned = {}
        x_grouped, w_grouped, a_grouped, h_grouped = {}, {}, {}, {}
        x_mx, w_mx, a_mx, h_mx = {}, {}, {}, {}
        b_t = {}
        lora_ps, base_ps, low_d_ps = {}, {}, {}
        lora_sb, gate_up, silu_gate, h_sb, h_rounded = {}, {}, {}, {}, {}

        def transpose_bank(shape, dtype):
            return ps.tile(shape, dtype, name="bank", tag="bank", bufs=8)

        def mx_tiles(name, columns, bufs=2):
            shape = [P, 2, columns]
            words = sb.tile(shape, U32, name=name + "_words", tag=name + "_words", bufs=bufs, align_bytes=64)
            scales = sb.tile(shape, U8, name=name + "_scales", tag=name + "_scales", bufs=bufs, align_bytes=64)
            return words, scales

        def quantise_both_passes(mx, grouped):
            words, scales = mx
            nc.vector.quantize_mx(
                out=words[:].rearrange("q g y -> q (g y)").bitcast(FP8X4),
                scales=scales[:].rearrange("q g y -> q (g y)"),
                in_=grouped[:].rearrange("q g y t -> q (g y t)"),
            )

        zeros = const.tile([P, N], BF16, name="zeros")
        nc.vector.memset(zeros[:], 0.0)

        def warm_up(n):
            for i in range(n):
                idle_ps = transpose_bank([P, N], F32)
                nc.tensor.matmul(idle_ps[:], lhsT=zeros[:, :P], rhs=zeros[:], start=True, stop=True)

        def load_chunk(c, pieces=1):
            if c >= CHUNKS:
                return
            e, js = divmod(c, 4)
            j, s = divmod(js, 2)
            w_raw[c] = sb.tile([P, 4, H], BF16, name="w_raw", tag="w_raw", bufs=CHUNK_BUFS)
            row = D * s + N * j
            rows = W_gu[e, row:row + N, :].rearrange("(p r) k -> p r k", r=4)
            size = 4 // pieces
            for r in range(0, 4, size):
                nc.sync.dma_start(out=w_raw[c][:, r:r + size, :], in_=rows[:, r:r + size, :])

        def load_x(e):
            if e >= E:
                return
            x_raw[e] = sb.tile([P, 2, H], BF16, name="x_raw", tag="x_raw")
            nc.sync.dma_start(out=x_raw[e][:], in_=x[e].rearrange("(p m) k -> p m k", m=2))

        def load_b(e, j):
            if e >= E:
                return
            b_raw[(e, j)] = sb.tile([P, 2, 4, R], BF16, name="b_raw", tag="b_raw", bufs=4)
            rows = B_gu[e].rearrange("(s j p r) y -> p s j r y", s=2, j=2, r=4)
            nc.sync.dma_start(out=b_raw[(e, j)][:], in_=rows[:, :, j, :, :])

        def load_a(e):
            if e >= E:
                return
            a_raw[e] = sb.tile([P, D], BF16, name="a_raw", tag="a_raw", bufs=A_BUFS)
            nc.sync.dma_start(out=a_raw[e][:], in_=A_d[e])

        def load_low(first, last):
            nc.sync.dma_start(
                out=low_raw[:, first:last, :, :], in_=low_gu[first:last].rearrange("e (p m) y -> p e m y", m=2)
            )

        def transpose_x(e, m):
            if e >= E:
                return
            pairs = x_raw[e][:].bitcast(F32)
            bank = transpose_bank([P, 2, 2, P], F32)
            for g in range(2):
                for u in range(2):
                    first = PAIRS_PASS * g + P * u
                    nc.tensor.transpose(bank[:, g, u, :], pairs[:, m, first:first + P], ident_f32[:])
            turned[("x", e, m)] = bank

        def regroup_x(e, m, copy):
            if e >= E:
                return
            if e not in x_grouped:
                x_grouped[e] = sb.tile([P, 2, T, 4], BF16, name="x_grouped", tag="x_grouped", align_bytes=64)
            copy(
                out=x_grouped[e][:].bitcast(F32)[:, :, m * P:(m + 1) * P, :],
                in_=turned[("x", e, m)][:].rearrange("q g u y -> q g y u"),
            )

        def quantise_x(e):
            if e >= E:
                return
            x_mx[e] = mx_tiles("x", T)
            quantise_both_passes(x_mx[e], x_grouped[e])

        def transpose_chunk(c, r):
            pairs = w_raw[c][:].bitcast(F32)
            bank = transpose_bank([P, 2, 2, P], F32)
            for g in range(2):
                for u in range(2):
                    first = PAIRS_PASS * g + P * u
                    nc.tensor.transpose(bank[:, g, u, :], pairs[:, r, first:first + P], ident_f32[:])
            turned[("w", c, r)] = bank

        def regroup_chunk(c, r, copy):
            if c not in w_grouped:
                w_grouped[c] = sb.tile([P, 2, N, 4], BF16, name="w_grouped", tag="w_grouped", bufs=3, align_bytes=64)
            copy(
                out=w_grouped[c][:].bitcast(F32)[:, :, r * P:(r + 1) * P, :],
                in_=turned[("w", c, r)][:].rearrange("q g u y -> q g y u"),
            )

        def quantise_chunk(c):
            w_mx[c] = mx_tiles("w", N, W_MX_BUFS)
            quantise_both_passes(w_mx[c], w_grouped[c])

        def transpose_b(e, j):
            if e >= E:
                return
            bank = transpose_bank([P, 2, N], BF16)
            for s in range(2):
                for r in range(4):
                    nc.tensor.transpose(bank[:, s, r * P:(r + 1) * P], b_raw[(e, j)][:, s, r, :], ident_bf16[:])
            turned[("b", e, j)] = bank

        def copy_b(e, j):
            if e >= E:
                return
            b_t[(e, j)] = sb.tile([P, 2, N], BF16, name="b_t", tag="b_t", bufs=3)
            nc.scalar.copy(out=b_t[(e, j)][:], in_=turned[("b", e, j)][:])

        def transpose_low(first, last):
            bank = transpose_bank([P, last - first, 2, P], BF16)
            for e in range(first, last):
                for m in range(2):
                    nc.tensor.transpose(bank[:, e - first, m, :], low_raw[:, e, m, :], ident_bf16[:])
            turned["low"] = bank

        def double_low(first, last):
            nc.scalar.mul(out=low_t[:, first:last, :, :], in_=turned["low"][:], mul=2.0)

        def transpose_a(e):
            pairs = a_raw[e][:].bitcast(F32)
            bank = transpose_bank([P, 2, 2, R], F32)
            for g in range(2):
                for u in range(2):
                    first = PAIRS_PASS * g + P * u
                    nc.tensor.transpose(bank[:, g, u, :], pairs[:, first:first + P], ident_f32[:])
            turned[("a", e)] = bank

        def regroup_a(e, copy):
            a_grouped[e] = sb.tile([P, 2, R, 4], BF16, name="a_grouped", tag="a_grouped", align_bytes=64)
            copy(out=a_grouped[e][:].bitcast(F32), in_=turned[("a", e)][:].rearrange("q g u y -> q g y u"))

        def quantise_a(e):
            a_mx[e] = mx_tiles("a", R, E)
            quantise_both_passes(a_mx[e], a_grouped[e])

        def lora_half(f, s, half):
            if f >= PHASES:
                return
            e, jm = divmod(f, 4)
            j, m = divmod(jm, 2)
            if half == 0:
                lora_ps[(f, s)] = ps.tile([P, N], F32, name="lora_ps", tag="bank", bufs=8)
            columns = slice(half * N // 2, (half + 1) * N // 2)
            nc.tensor.matmul(
                lora_ps[(f, s)][:, columns],
                lhsT=low_t[:, e, m, :],
                rhs=b_t[(e, j)][:, s, columns],
                start=True,
                stop=True,
            )

        def copy_lora(f, s):
            if f >= PHASES:
                return
            lora_sb[(f, s)] = sb.tile([P, N], F32, name="lora_sb", tag="lora_sb", bufs=LORA_BUFS)
            nc.scalar.copy(
                out=lora_sb[(f, s)][:].rearrange("z (p r) -> z p r", r=4),
                in_=lora_ps[(f, s)][:].rearrange("z (r p) -> z p r", r=4),
            )

        def base_matmul(f, s, spare_bank=False):
            e, jm = divmod(f, 4)
            m = jm % 2
            x_words, x_scales = x_mx[e]
            w_words, w_scales = w_mx[2 * (f // 2) + s]
            if spare_bank:
                base_ps[(f, s)] = transpose_bank([P, N], F32)
            else:
                base_ps[(f, s)] = ps.tile([P, N], F32, name="base_ps", tag="bank", bufs=8)
            for g in range(2):
                nc.tensor.matmul_mx(
                    out=base_ps[(f, s)][:],
                    lhsT=x_words[:, g, m * P:(m + 1) * P].bitcast(FP8X4),
                    lhsT_scale=x_scales[:, g, m * P:(m + 1) * P],
                    rhs=w_words[:, g, :].bitcast(FP8X4),
                    rhs_scale=w_scales[:, g, :],
                    start=(g == 0),
                    stop=(g == 1),
                )

        def add_lora(f, s):
            if f < 0:
                return
            gate_up[(f, s)] = sb.tile([P, N], F32, name="gate_up", tag="gate_up%d" % s, bufs=GU_BUFS)
            nc.vector.tensor_tensor(
                out=gate_up[(f, s)][:].rearrange("z (p r) -> z p r", r=4),
                in0=lora_sb[(f, s)][:].rearrange("z (p r) -> z p r", r=4),
                in1=base_ps[(f, s)][:].rearrange("z (r p) -> z p r", r=4),
                op=ADD,
            )

        def silu(f):
            if f < 0:
                return
            silu_gate[f] = sb.tile([P, N], F32, name="silu_gate", tag="silu_gate", bufs=GU_BUFS)
            nc.scalar.activation(out=silu_gate[f][:], in_=gate_up[(f, 0)][:], func=SILU)

        def h_rounded_tile(f):
            t, m = divmod(f, 2)
            if t not in h_sb:
                h_sb[t] = sb.tile([P, 2, N], F32, name="h_sb", tag="h_sb", bufs=5)
                h_rounded[t] = sb.tile([P, 2, N], BF16, name="h_rounded", tag="h_rounded", bufs=2)
            return h_rounded[t][:, m, :]

        def store_h_half(f):
            t, m = divmod(f, 2)
            e, j = divmod(t, 2)
            nc.sync.dma_start(
                out=out_0[e, :, N * j:N * (j + 1)].rearrange("(p m) d -> m p d", m=2)[m], in_=h_sb[t][:, m, :]
            )

        def product(f, engine):
            if f < 0:
                return
            m = f % 2
            h_rounded_tile(f)
            engine.tensor_tensor(
                out=h_sb[f // 2][:, m, :], in0=gate_up[(f, 1)][:], in1=silu_gate[f][:], op=MULT
            )

        def round_h(f):
            if f < 0:
                return
            m = f % 2
            nc.gpsimd.tensor_scalar(
                out=h_rounded[f // 2][:, m, :],
                in0=h_sb[f // 2][:, m, :],
                scalar1=1.0,
                scalar2=0.0,
                op0=MULT,
                op1=ADD,
            )

        def store_h(f):
            if f < 0 or f % 2 == 0:
                return
            e, j = divmod(f // 2, 2)
            nc.sync.dma_start(
                out=out_0[e, :, N * j:N * (j + 1)].rearrange("(p m) d -> p m d", m=2), in_=h_sb[f // 2][:]
            )

        def transpose_h(pair, tokens=(0, 1)):
            if pair < 0:
                return
            bank = transpose_bank([P, len(tokens), 2, P], F32)
            for i, m in enumerate(tokens):
                pairs = h_rounded[pair][:].bitcast(F32)
                for u in range(2):
                    nc.tensor.transpose(bank[:, i, u, :], pairs[:, m, u * P:(u + 1) * P], ident_f32[:])
            turned[("h", pair, tokens)] = bank

        def regroup_h(pair, tokens=(0, 1), copy=None):
            if pair < 0:
                return
            if pair not in h_grouped:
                h_grouped[pair] = sb.tile([P, T, 4], BF16, name="h_grouped", tag="h_grouped", align_bytes=64)
            first, last = tokens[0] * P, (tokens[-1] + 1) * P
            (copy or nc.scalar.copy)(
                out=h_grouped[pair][:].bitcast(F32)[:, first:last, :].rearrange("q (m y) u -> q m y u", y=P),
                in_=turned[("h", pair, tokens)][:].rearrange("q m u y -> q m y u"),
            )

        def quantise_h(pair, tokens=(0, 1)):
            if pair < 0:
                return
            e, j = divmod(pair, 2)
            if e not in h_mx:
                h_mx[e] = mx_tiles("h", T)
            words, scales = h_mx[e]
            first, last = tokens[0] * P, (tokens[-1] + 1) * P
            nc.vector.quantize_mx(
                out=words[:, j, first:last].bitcast(FP8X4),
                scales=scales[:, j, first:last],
                in_=h_grouped[pair][:, first:last, :].rearrange("q y t -> q (y t)"),
            )

        def low_d_matmul(e):
            if e < 0:
                return
            h_words, h_scales = h_mx[e]
            a_words, a_scales = a_mx[e]
            low_d_ps[e] = transpose_bank([P, 2, R], F32)
            for m in range(2):
                for g in range(2):
                    nc.tensor.matmul_mx(
                        out=low_d_ps[e][:, m, :],
                        lhsT=h_words[:, g, m * P:(m + 1) * P].bitcast(FP8X4),
                        lhsT_scale=h_scales[:, g, m * P:(m + 1) * P],
                        rhs=a_words[:, g, :].bitcast(FP8X4),
                        rhs_scale=a_scales[:, g, :],
                        start=(g == 0),
                        stop=(g == 1),
                    )

        def store_low_d(e):
            if e < 0:
                return
            low_d_sb = sb.tile([P, 2, R], F32, name="low_d_sb", tag="low_d_sb")
            copy = on_s if e == E - 1 else on_v
            copy(out=low_d_sb[:], in_=low_d_ps[e][:])
            nc.sync.dma_start(out=out_1[e].rearrange("(p m) y -> p m y", m=2), in_=low_d_sb[:])

        on_v = nc.vector.tensor_copy
        on_s = nc.scalar.copy

        load_chunk(0, 2)
        load_x(0)
        load_low(0, 1)
        load_b(0, 0)
        load_chunk(1, 2)
        load_chunk(2)
        load_b(0, 1)
        load_chunk(3)
        load_x(1)
        load_chunk(4)
        load_b(1, 0)
        load_low(1, E)
        load_b(1, 1)
        load_a(0)
        for c in range(5, CHUNK_BUFS + 1):
            load_chunk(c)
        warm_up(5)
        for r in range(4):
            transpose_chunk(0, r)
            regroup_chunk(0, r, on_v if r % 2 == 0 else on_s)
            if r % 2 == 1:
                warm_up(1)
        for m in range(2):
            transpose_x(0, m)
        warm_up(1)
        quantise_chunk(0)
        regroup_x(0, 0, on_s)
        regroup_x(0, 1, on_s)
        transpose_low(0, 1)
        double_low(0, 1)
        transpose_b(0, 0)
        warm_up(1)
        copy_b(0, 0)
        quantise_x(0)
        for r in range(4):
            transpose_chunk(1, r)
            regroup_chunk(1, r, on_v if r % 2 == 0 else on_s)
            if r == 1:
                warm_up(1)
        lora_half(0, 0, 0)
        lora_half(0, 0, 1)
        base_matmul(0, 0)
        lora_half(1, 0, 0)
        lora_half(1, 0, 1)
        copy_lora(0, 0)
        lora_half(0, 1, 0)
        lora_half(0, 1, 1)
        copy_lora(0, 1)
        quantise_chunk(1)
        add_lora(0, 0)

        for f in range(PHASES - 2):
            c = f + CHUNK_LEAD
            e, in_expert = divmod(f, 4)
            next_e = e + 1
            if in_expert == 0:
                load_x(e + 2)
            if in_expert == 1:
                load_b(e + 2, 0)
                load_b(e + 2, 1)
            if f in (2, 6, 7):
                load_a(1 + (2, 6, 7).index(f))
            load_chunk(c + CHUNK_BUFS - 1)
            transpose_chunk(c, 0)
            transpose_chunk(c, 1)
            add_lora(f - 1, 1)
            if f % 2 == 0:
                quantise_h((f - 4) // 2)
            if in_expert == 3:
                quantise_x(e + 1)
            if f - 1 in A_PHASES:
                quantise_a(A_PHASES.index(f - 1))
            if f > 0:
                quantise_chunk(c - 1)
            silu(f - 1)
            product(f - 1, nc.gpsimd)
            round_h(f - 1)
            store_h(f - 5)
            regroup_chunk(c, 0, on_s)
            if f > 0:
                lora_half(f + 1, 0, 0)
                base_matmul(f, 0)
                lora_half(f + 1, 0, 1)
            regroup_chunk(c, 1, on_v)
            copy_lora(f + 1, 0)
            if f == 2:
                transpose_low(1, E)
                double_low(1, E)
            if f % 2 == 1:
                transpose_h((f - 3) // 2)
                regroup_h((f - 3) // 2)
            else:
                b_e, b_j = divmod((f + 2) // 2, 2)
                transpose_b(b_e, b_j)
                copy_b(b_e, b_j)
            if in_expert in (1, 2):
                transpose_x(e + 1, in_expert - 1)
                regroup_x(e + 1, in_expert - 1, on_s)
            if f in A_PHASES:
                transpose_a(A_PHASES.index(f))
                regroup_a(A_PHASES.index(f), on_s)
            transpose_chunk(c, 2)
            transpose_chunk(c, 3)
            if f > 0:
                add_lora(f, 0)
            regroup_chunk(c, 2, on_v)
            regroup_chunk(c, 3, on_s)
            lora_half(f + 1, 1, 0)
            if in_expert == 2:
                low_d_matmul(e - 1)
            base_matmul(f, 1)
            lora_half(f + 1, 1, 1)
            copy_lora(f + 1, 1)
            if in_expert == 2:
                store_low_d(e - 1)

        f = PHASES - 2
        add_lora(f - 1, 1)
        quantise_h((f - 4) // 2)
        quantise_chunk(CHUNKS - 1)
        silu(f - 1)
        for s in range(2):
            lora_half(f + 1, s, 0)
            lora_half(f + 1, s, 1)
            copy_lora(f + 1, s)
        base_matmul(f, 0)
        base_matmul(f + 1, 0, spare_bank=True)
        product(f - 1, nc.gpsimd)
        round_h(f - 1)
        for t in (5, 3, 1):
            store_h(f - t)
        add_lora(f, 0)
        silu(f)
        add_lora(f + 1, 0)
        silu(f + 1)
        base_matmul(f, 1)
        base_matmul(f + 1, 1, spare_bank=True)
        low_d_matmul(E - 2)
        add_lora(f, 1)
        add_lora(f + 1, 1)
        for m in range(2):
            nc.vector.tensor_tensor(
                out=h_rounded_tile(f + m), in0=gate_up[(f + m, 1)][:], in1=silu_gate[f + m][:], op=MULT
            )
        product(f, nc.vector)
        store_h_half(f)
        transpose_h((f - 2) // 2)
        regroup_h((f - 2) // 2)
        for m in range(2):
            transpose_h(f // 2, (m,))
            regroup_h(f // 2, (m,))
        store_low_d(E - 2)
        quantise_h((f - 2) // 2)
        for m in range(2):
            quantise_h(f // 2, (m,))
        product(f + 1, nc.vector)
        store_h_half(f + 1)
        low_d_matmul(E - 1)
        store_low_d(E - 1)
